import numpy as np
import ml_dtypes


def mxq(x, axis, fmt="e4m3"):
    dtype, down = {"e4m3": (ml_dtypes.float8_e4m3fn, 7), "e5m2": (ml_dtypes.float8_e5m2, 14)}[fmt]
    v = np.moveaxis(np.asarray(x, np.float32).astype(ml_dtypes.bfloat16).astype(np.float64), axis, -1)
    blocks = v.reshape(v.shape[:-1] + (-1, 32))
    amax = np.abs(blocks).max(-1, keepdims=True)
    byte = np.maximum(np.where(amax > 0, np.frexp(amax)[1] - 1 + 127, 0) - down, 1)
    scale = np.exp2(byte - 127.0)
    codes = (blocks / scale).astype(np.float32).astype(dtype).astype(np.float64)
    return np.moveaxis((codes * scale).reshape(v.shape), -1, axis)


WIDE = False


def mx_kscale(k):
    if not WIDE:
        return np.ones(k)
    levels = np.array([10, -10, 5, -5, 0])
    a = np.random.permutation(np.resize(levels, k // 512 * 4)).reshape(k // 512, 4)
    idx = np.arange(k)
    return np.exp2(a[idx // 512, idx % 128 // 32])


BF16 = ml_dtypes.bfloat16


def bf(x):
    return np.asarray(x, np.float32).astype(BF16)


def f64(x):
    return np.asarray(x).astype(np.float64)


E2M1 = np.array([0.0, 0.5, 1.0, 1.5, 2.0, 3.0, 4.0, 6.0, -0.0, -0.5, -1.0, -1.5, -2.0, -3.0, -4.0, -6.0])


def pack_weight(w, fmt):
    k, n = w.shape
    w = f64(bf(w)).reshape(k // 32, 32, n)
    amax = np.abs(w).max(1)
    if fmt == "e4m3":
        byte = np.frexp(amax)[1] - 1 + 127 - 7
    else:
        mant, ex = np.frexp(amax / 6.0)
        byte = np.where(mant > 0.5, ex, ex - 1) + 127
    byte = np.clip(np.where(amax > 0, byte, 1), 1, 254)
    scaled = (w * np.exp2(127.0 - byte)[:, None, :]).reshape(k, n).astype(np.float32)
    by_word = np.ascontiguousarray(scaled.reshape(k // 512, 128, 4, n).transpose(0, 1, 3, 2))
    if fmt == "e4m3":
        words = by_word.astype(ml_dtypes.float8_e4m3fn).view(np.uint8)
    else:
        c = by_word.astype(ml_dtypes.float4_e2m1fn).view(np.uint8) & 0xF
        words = c[..., 0::2] | (c[..., 1::2] << 4)
    return np.ascontiguousarray(words), np.ascontiguousarray(byte.astype(np.uint8).reshape(k // 512, 16, n))


def unpack_weight(words, scales, fmt):
    g, p, n, _ = words.shape
    if fmt == "e4m3":
        vals = np.ascontiguousarray(words).view(ml_dtypes.float8_e4m3fn).astype(np.float64)
    else:
        nib = np.empty((g, p, n, 4), np.uint8)
        nib[..., 0::2] = words & 0xF
        nib[..., 1::2] = words >> 4
        vals = E2M1[nib]
    vals = vals * np.repeat(np.exp2(scales.astype(np.float64) - 127.0), 8, axis=1)[..., None]
    return vals.transpose(0, 1, 3, 2).reshape(g * 512, n)


B, I, J, P, D = 8, 512, 512, 32, 8
EPS = 1e-5
FMT = "e4m3"


def stdz(t):
    m = t.mean(axis=(-1, -2), keepdims=True)
    s = t.std(axis=(-1, -2), keepdims=True, ddof=1)
    return (t - m) / (s + EPS)


def flat_softmax(t):
    e = np.exp(t - t.max(axis=(-1, -2), keepdims=True))
    return e / e.sum(axis=(-1, -2), keepdims=True)


def setup_inputs():
    s = mx_kscale(J)
    x = bf((np.random.standard_normal((B, I, J)) + 0.25) * s)
    o_stack = (np.random.standard_normal((D, J, P)) * 2.0 / np.sqrt(J + P) + 2.0 / J) / s[:, None]
    p_stack = np.random.standard_normal((D, I, P)) * 2.0 / np.sqrt(I + P)
    rel_stack = np.random.standard_normal((D, J, P)) * 2.0 / np.sqrt(J + P) / s[:, None]
    o_words, o_scales = pack_weight(o_stack.reshape(-1, P), FMT)
    p_words, p_scales = pack_weight(p_stack.reshape(-1, P), FMT)
    rel_words, rel_scales = pack_weight(rel_stack.reshape(-1, P), FMT)
    return {"x": x,
            "o_xj_words": o_words, "o_xj_scales": o_scales,
            "p_xj_words": p_words, "p_xj_scales": p_scales,
            "rel_o_xj_words": rel_words, "rel_o_xj_scales": rel_scales}


def reference(x, o_xj_words, o_xj_scales, p_xj_words, p_xj_scales, rel_o_xj_words, rel_o_xj_scales):
    xq = mxq(f64(x), 2, "e4m3")[:, None]
    mass = flat_softmax(xq @ unpack_weight(rel_o_xj_words, rel_o_xj_scales, FMT).reshape(D, J, P)).sum(-2)
    t = stdz(np.tanh(xq @ unpack_weight(o_xj_words, o_xj_scales, FMT).reshape(D, J, P)))
    u = mxq(t, 2, "e4m3").transpose(0, 1, 3, 2) @ unpack_weight(p_xj_words, p_xj_scales, FMT).reshape(D, I, P)
    return stdz(np.tanh(u)), mass

@@ -1,0 +1,470 @@
+from contextlib import ExitStack
+
+import concourse.mybir as mybir
+from concourse.masks import make_identity
+
+F32 = mybir.dt.float32
+BF16 = mybir.dt.bfloat16
+I32 = mybir.dt.int32
+U32 = mybir.dt.uint32
+U8 = mybir.dt.uint8
+FP8X4 = mybir.dt.float8_e4m3fn_x4
+ACT = mybir.ActivationFunctionType
+ALU = mybir.AluOpType
+AXIS = mybir.AxisListType
+
+P = 128
+PACK = 4
+QUADRANT = 32
+
+BATCH = 8
+ROWS = 512
+COLS = 512
+DEPTHS = 8
+WIDTH = 32
+EPS = 1e-5
+
+ALL_WIDTH = DEPTHS * WIDTH
+HALVES = ALL_WIDTH // P
+DEPTHS_PER_HALF = DEPTHS // HALVES
+WORDS = COLS // 2
+GROUP = P // WIDTH
+PAIR_WIDTH = 2 * WIDTH
+SET_PAIRS = PACK // 2
+PIECE = ROWS // SET_PAIRS
+
+LAG = 4
+
+FLOPS = 2 * BATCH * DEPTHS * (2 * ROWS * COLS * WIDTH + ROWS * WIDTH * WIDTH)
+
+
+def tile_selfprojectiondev_pa_e_kernel(
+    tc,
+    x,
+    o_xj_words,
+    o_xj_scales,
+    p_xj_words,
+    p_xj_scales,
+    rel_o_xj_words,
+    rel_o_xj_scales,
+    out_0,
+    out_1,
+):
+    nc = tc.nc
+    with ExitStack() as stack:
+        stack.enter_context(tc.manual_schedule())
+        const = stack.enter_context(tc.tile_pool(name="const", bufs=1))
+        x_pool = stack.enter_context(tc.tile_pool(name="x_pool", bufs=BATCH))
+        work = stack.enter_context(tc.tile_pool(name="work", bufs=4))
+        small = stack.enter_context(tc.tile_pool(name="small", bufs=4))
+        group_pool = stack.enter_context(tc.tile_pool(name="group_pool", bufs=2))
+        psum_flip = stack.enter_context(tc.psum_pool(name="psum_flip", bufs=SET_PAIRS))
+        psum_first = stack.enter_context(tc.psum_pool(name="psum_first", bufs=2 * HALVES))
+        psum_one = stack.enter_context(tc.psum_pool(name="psum_one", bufs=1))
+
+        identity = const.tile([P, P], F32)
+        make_identity(nc, identity[:])
+        averager = const.tile([P, P], F32)
+        nc.vector.memset(averager[:], 1.0 / (ROWS * WIDTH))
+        half = const.tile([P, DEPTHS], F32)
+        nc.vector.memset(half[:], 0.5)
+
+        planes = const.tile([P, 3, ALL_WIDTH], U8, align_bytes=64)
+        nc.vector.memset(planes[:].rearrange("q k n -> q (k n)").bitcast(I32), 0)
+        o_plane, rel_plane, p_plane = planes[:, 0, :], planes[:, 1, :], planes[:, 2, :]
+        o_codes = const.tile([P, ALL_WIDTH], U32, align_bytes=64)
+        rel_codes = const.tile([P, ALL_WIDTH], U32, align_bytes=64)
+        p_codes = const.tile([P, ALL_WIDTH], U32, align_bytes=64)
+
+        def load_codes(codes, words):
+            nc.sync.dma_start(
+                out=codes[:].bitcast(I32).rearrange("q (d n) -> q d n", d=DEPTHS),
+                in_=words.rearrange("d q n t -> q d (n t)").bitcast(I32),
+            )
+
+        def load_scales(plane, scales):
+            for quad in range(P // QUADRANT):
+                nc.sync.dma_start(
+                    out=plane[QUADRANT * quad : QUADRANT * quad + PACK, :]
+                    .bitcast(I32)
+                    .rearrange("r (d n) -> r d n", d=DEPTHS),
+                    in_=scales[:, PACK * quad : PACK * (quad + 1), :]
+                    .rearrange("d r n -> r d n")
+                    .bitcast(I32),
+                )
+
+        x_rows = {}
+
+        def load_x(b):
+            x_rows[b] = x_pool.tile([P, PACK, COLS], BF16, name="x_rows")
+            by_set = x[b].rearrange("(q a) j -> q a j", a=PACK)
+            for piece in range(SET_PAIRS):
+                sets = slice(2 * piece, 2 * piece + 2)
+                nc.sync.dma_start(out=x_rows[b][:, sets, :], in_=by_set[:, sets, :])
+
+        load_x(0)
+        load_codes(o_codes, o_xj_words)
+        load_scales(o_plane, o_xj_scales)
+        load_x(1)
+        load_x(2)
+        load_codes(rel_codes, rel_o_xj_words)
+        load_scales(rel_plane, rel_o_xj_scales)
+        load_x(3)
+        load_codes(p_codes, p_xj_words)
+        load_scales(p_plane, p_xj_scales)
+        for b in range(4, BATCH):
+            load_x(b)
+
+        def exists(b):
+            return 0 <= b < BATCH
+
+        flipped = {}
+        x_grouped = {}
+        x_codes = {}
+        x_scales = {}
+
+        def transpose_x(b, piece):
+            if not exists(b):
+                return
+            words = x_rows[b][:].rearrange("q a j -> q (a j)").bitcast(F32)
+            flipped[(b, piece)] = psum_flip.tile([P, 2, PIECE], F32, name="flipped")
+            for a2 in range(2):
+                a = 2 * piece + a2
+                for u in range(2):
+                    nc.tensor.transpose(
+                        flipped[(b, piece)][:, u, a2 * P : (a2 + 1) * P],
+                        words[:, a * WORDS + u : (a + 1) * WORDS : 2],
+                        identity[:],
+                    )
+
+        def regroup_x(b, piece):
+            if not exists(b):
+                return
+            x_grouped[(b, piece)] = work.tile([P, PIECE, PACK], BF16, name="x_grouped", align_bytes=64)
+            nc.vector.tensor_copy(
+                out=x_grouped[(b, piece)][:]
+                .rearrange("k c t -> k (c t)")
+                .bitcast(F32)
+                .rearrange("k (c u) -> k c u", u=2),
+                in_=flipped[(b, piece)][:].rearrange("k u c -> k c u"),
+            )
+
+        def quantise_x(b, piece):
+            if not exists(b):
+                return
+            if piece == 0:
+                x_codes[b] = x_pool.tile([P, ROWS], U32, name="x_codes", align_bytes=64)
+                x_scales[b] = x_pool.tile([P, ROWS], U8, name="x_scales", align_bytes=64)
+            rows = slice(piece * PIECE, (piece + 1) * PIECE)
+            nc.vector.quantize_mx(
+                out=x_codes[b][:, rows].bitcast(FP8X4),
+                scales=x_scales[b][:, rows],
+                in_=x_grouped[(b, piece)][:].rearrange("k c t -> k (c t)"),
+            )
+
+        z = {}
+        r = {}
+
+        def project_o(b):
+            if not exists(b):
+                return
+            for h in range(HALVES):
+                z[(b, h)] = psum_first.tile([P, PACK, P], F32, name="z", tag="first")
+            for a in range(PACK):
+                row_set = slice(a * P, (a + 1) * P)
+                for h in range(HALVES):
+                    cols = slice(h * P, (h + 1) * P)
+                    nc.tensor.matmul_mx(
+                        out=z[(b, h)][:, a, :],
+                        lhsT=x_codes[b][:, row_set].bitcast(FP8X4),
+                        lhsT_scale=x_scales[b][:, row_set],
+                        rhs=o_codes[:, cols].bitcast(FP8X4),
+                        rhs_scale=o_plane[:, cols],
+                        start=True,
+                        stop=True,
+                    )
+
+        def project_rel(b):
+            if not exists(b):
+                return
+            for h in range(HALVES):
+                cols = slice(h * P, (h + 1) * P)
+                r[(b, h)] = psum_first.tile([P, ROWS], F32, name="r", tag="first")
+                nc.tensor.matmul_mx(
+                    out=r[(b, h)][:],
+                    lhsT=rel_codes[:, cols].bitcast(FP8X4),
+                    lhsT_scale=rel_plane[:, cols],
+                    rhs=x_codes[b][:].bitcast(FP8X4),
+                    rhs_scale=x_scales[b][:],
+                    start=True,
+                    stop=True,
+                )
+
+        neg_max = const.tile([P, QUADRANT], F32, align_bytes=64)
+        nc.vector.memset(neg_max[:], 0.0)
+        exp_sum = const.tile([P, QUADRANT], F32, align_bytes=64)
+        nc.vector.memset(exp_sum[:], 1.0)
+
+        def row_max(b):
+            if not exists(b):
+                return
+            for h in range(HALVES):
+                c = HALVES * b + h
+                nc.vector.tensor_reduce(
+                    out=neg_max[:, c : c + 1], in_=r[(b, h)][:], axis=AXIS.X, op=ALU.max, negate=True
+                )
+
+        def row_exp_sum(b):
+            if not exists(b):
+                return
+            for h in range(HALVES):
+                c = HALVES * b + h
+                unread = work.tile([P, ROWS], BF16, name="unread_exp")
+                nc.scalar.activation(
+                    out=unread[:],
+                    in_=r[(b, h)][:],
+                    func=ACT.Exp,
+                    bias=neg_max[:, c : c + 1],
+                    accum_out=exp_sum[:, c : c + 1],
+                )
+
+        def store_mass(b):
+            if b != BATCH - 1:
+                return
+            neg_max_t = const.tile([P, QUADRANT], F32, align_bytes=64)
+            nc.vector.transpose(out=neg_max_t[:], in_=neg_max[:])
+            neg_top = const.tile([P, 1], F32)
+            nc.vector.tensor_reduce(out=neg_top[:], in_=neg_max_t[:], axis=AXIS.X, op=ALU.min)
+            rescale = const.tile([P, WIDTH], F32)
+            nc.scalar.activation(
+                out=rescale[:], in_=neg_max_t[:], func=ACT.Exp, bias=neg_top[:], scale=-1.0
+            )
+            exp_sum_t = const.tile([P, QUADRANT], F32, align_bytes=64)
+            nc.vector.transpose(out=exp_sum_t[:], in_=exp_sum[:])
+            unnormalised = const.tile([P, WIDTH], F32)
+            nc.vector.tensor_mul(out=unnormalised[:], in0=rescale[:], in1=exp_sum_t[:])
+            denominator = const.tile([P, 1], F32)
+            nc.vector.reduce_sum(out=denominator[:], in_=unnormalised[:], axis=AXIS.X)
+            nc.vector.reciprocal(out=denominator[:], in_=denominator[:])
+            mass = const.tile([P, WIDTH], F32)
+            nc.vector.tensor_scalar_mul(out=mass[:], in0=unnormalised[:], scalar1=denominator[:])
+            by_depth = out_1.rearrange("b (h k) w -> k (b h) w", k=DEPTHS_PER_HALF)
+            for k in range(DEPTHS_PER_HALF):
+                nc.sync.dma_start(
+                    out=by_depth[k], in_=mass[QUADRANT * k : QUADRANT * k + HALVES * BATCH, :]
+                )
+
+        def std_plus_eps(mean, mean_of_squares, count):
+            shape = [P, mean.shape[1]]
+            var = small.tile(shape, F32, name="var")
+            nc.gpsimd.tensor_tensor(out=var[:], in0=mean, in1=mean, op=ALU.mult)
+            nc.gpsimd.tensor_tensor(out=var[:], in0=mean_of_squares, in1=var[:], op=ALU.subtract)
+            nc.gpsimd.tensor_scalar(
+                out=var[:], in0=var[:], scalar1=count / (count - 1.0), scalar2=0.0,
+                op0=ALU.mult, op1=ALU.max,
+            )
+            std = small.tile(shape, F32, name="std")
+            nc.gpsimd.tensor_tensor(out=std[:], in0=var[:], in1=half[:, 0 : shape[1]], op=ALU.pow)
+            nc.gpsimd.tensor_scalar_add(out=std[:], in0=std[:], scalar1=EPS)
+            return std
+
+        tanh_z = {}
+        sums = {}
+        averages = {}
+        t_moments = {}
+        t_std = {}
+        t_grouped = {}
+
+        def tanh_of_z(b):
+            if not exists(b):
+                return
+            tanh_z[b] = work.tile([P, DEPTHS, WIDTH * PACK], F32, name="tanh_z")
+            sums[b] = small.tile([P, 2 * DEPTHS], F32, name="sums")
+            for d in range(DEPTHS):
+                h, k = divmod(d, DEPTHS_PER_HALF)
+                nc.scalar.activation(
+                    out=tanh_z[b][:, d, :].rearrange("q (w a) -> q w a", a=PACK),
+                    in_=z[(b, h)][:, :, k * WIDTH : (k + 1) * WIDTH].rearrange("q a w -> q w a"),
+                    func=ACT.Tanh,
+                    accum_out=sums[b][:, d : d + 1],
+                )
+
+        def squares_of_tanh(b):
+            if not exists(b):
+                return
+            for d in range(DEPTHS):
+                unread = work.tile([P, WIDTH * PACK], BF16, name="unread_square")
+                nc.scalar.activation(
+                    out=unread[:],
+                    in_=tanh_z[b][:, d, :],
+                    func=ACT.Square,
+                    accum_out=sums[b][:, DEPTHS + d : DEPTHS + d + 1],
+                )
+
+        def average_over_partitions(b):
+            if not exists(b):
+                return
+            averages[b] = psum_one.tile([P, 2 * DEPTHS], F32, name="averages")
+            nc.tensor.matmul(out=averages[b][:], lhsT=averager[:], rhs=sums[b][:], start=True, stop=True)
+
+        def t_statistics(b):
+            if not exists(b):
+                return
+            t_moments[b] = small.tile([P, 2 * DEPTHS], F32, name="t_moments")
+            nc.vector.tensor_copy(out=t_moments[b][:], in_=averages[b][:])
+            t_std[b] = std_plus_eps(
+                t_moments[b][:, 0:DEPTHS], t_moments[b][:, DEPTHS : 2 * DEPTHS], ROWS * WIDTH
+            )
+
+        def standardise_t(b):
+            if not exists(b):
+                return
+            group, member = divmod(b, GROUP)
+            if member == 0:
+                t_grouped[group] = group_pool.tile(
+                    [P, DEPTHS, GROUP, WIDTH * PACK], BF16, name="t_grouped", align_bytes=64
+                )
+            inv = small.tile([P, DEPTHS], F32, name="t_inv")
+            nc.vector.reciprocal(out=inv[:], in_=t_std[b][:])
+            for d in range(DEPTHS):
+                nc.vector.tensor_scalar(
+                    out=t_grouped[group][:, d, member, :],
+                    in0=tanh_z[b][:, d, :],
+                    scalar1=t_moments[b][:, d : d + 1],
+                    scalar2=inv[:, d : d + 1],
+                    op0=ALU.subtract,
+                    op1=ALU.mult,
+                )
+
+        u = {}
+        tanh_u = {}
+        squares_u = {}
+        centred_u = {}
+        u_std = {}
+        u_row_sums = {}
+        for moment in range(2):
+            u_row_sums[moment] = const.tile([P, QUADRANT], F32, name="u_row_sums%d" % moment, align_bytes=64)
+            nc.vector.memset(u_row_sums[moment][:], 0.0)
+
+        def closes_group(b):
+            return exists(b) and b % GROUP == GROUP - 1
+
+        def second_product(b):
+            if not closes_group(b):
+                return
+            group = b // GROUP
+            t_codes = group_pool.tile([P, DEPTHS * P], U32, name="t_codes", align_bytes=64)
+            t_scales = group_pool.tile([P, DEPTHS * P], U8, name="t_scales", align_bytes=64)
+            u[group] = psum_one.tile([P, DEPTHS, PAIR_WIDTH], F32, name="u")
+            for h in range(HALVES):
+                depths = slice(h * DEPTHS_PER_HALF, (h + 1) * DEPTHS_PER_HALF)
+                cols = slice(h * DEPTHS_PER_HALF * P, (h + 1) * DEPTHS_PER_HALF * P)
+                nc.vector.quantize_mx(
+                    out=t_codes[:, cols].bitcast(FP8X4),
+                    scales=t_scales[:, cols],
+                    in_=t_grouped[group][:, depths, :, :].rearrange("q d m e -> q (d m e)"),
+                )
+            for d in range(DEPTHS):
+                members = slice(d * P, (d + 1) * P)
+                pair = slice((d // 2) * PAIR_WIDTH, (d // 2 + 1) * PAIR_WIDTH)
+                nc.tensor.matmul_mx(
+                    out=u[group][:, d, :],
+                    lhsT=t_codes[:, members].bitcast(FP8X4),
+                    lhsT_scale=t_scales[:, members],
+                    rhs=p_codes[:, pair].bitcast(FP8X4),
+                    rhs_scale=p_plane[:, pair],
+                    start=True,
+                    stop=True,
+                )
+
+        def tanh_of_u(b):
+            if not closes_group(b):
+                return
+            group = b // GROUP
+            own = u[group][:].rearrange("q (e f) (g v) -> q e (f g) v", f=2, g=2)[:, :, 0:4:3, :]
+            tanh_u[group] = group_pool.tile([P, DEPTHS, WIDTH], F32, name="tanh_u")
+            nc.scalar.activation(
+                out=tanh_u[group][:].rearrange("q (e f) v -> q e f v", f=2), in_=own, func=ACT.Tanh
+            )
+            squares_u[group] = group_pool.tile([P, DEPTHS, WIDTH], F32, name="squares_u")
+            nc.scalar.activation(out=squares_u[group][:], in_=tanh_u[group][:], func=ACT.Square)
+
+        def spread_over_member(column):
+            repeated = small.tile([P, QUADRANT], F32, name="repeated", align_bytes=64)
+            nc.vector.tensor_copy(out=repeated[:], in_=column[:].to_broadcast([P, QUADRANT]))
+            spread = small.tile([P, QUADRANT], F32, name="spread", align_bytes=64)
+            nc.vector.transpose(out=spread[:], in_=repeated[:])
+            return spread[:, 0:DEPTHS].unsqueeze(2).to_broadcast([P, DEPTHS, WIDTH])
+
+        def u_statistics(b):
+            if not closes_group(b):
+                return
+            group = b // GROUP
+            by_depth = {}
+            moments = {}
+            for moment, values in enumerate((tanh_u[group], squares_u[group])):
+                nc.vector.reduce_sum(out=u_row_sums[moment][:, 0:DEPTHS], in_=values[:], axis=AXIS.X)
+            for moment in range(2):
+                by_depth[moment] = small.tile([P, QUADRANT], F32, name="by_depth", align_bytes=64)
+                nc.vector.transpose(out=by_depth[moment][:], in_=u_row_sums[moment][:])
+            for moment in range(2):
+                moments[moment] = small.tile([P, 1], F32, name="u_moment")
+                nc.vector.tensor_scalar(
+                    out=by_depth[moment][:], in0=by_depth[moment][:],
+                    scalar1=1.0 / (WIDTH * WIDTH), scalar2=None, op0=ALU.mult, op1=ALU.add,
+                    accum_out=moments[moment][:],
+                )
+            u_std[group] = std_plus_eps(moments[0][:], moments[1][:], WIDTH * WIDTH)
+            centred_u[group] = group_pool.tile([P, DEPTHS, WIDTH], F32, name="centred_u")
+            nc.vector.tensor_sub(
+                out=centred_u[group][:], in0=tanh_u[group][:], in1=spread_over_member(moments[0])
+            )
+
+        def store_proj(b):
+            if not closes_group(b):
+                return
+            group = b // GROUP
+            inv = small.tile([P, 1], F32, name="u_inv")
+            nc.vector.reciprocal(out=inv[:], in_=u_std[group][:])
+            proj = group_pool.tile([P, DEPTHS, WIDTH], F32, name="proj")
+            nc.vector.tensor_mul(out=proj[:], in0=centred_u[group][:], in1=spread_over_member(inv))
+            for member in range(GROUP):
+                nc.sync.dma_start(
+                    out=out_0[group * GROUP + member].rearrange("d w v -> w d v"),
+                    in_=proj[member * WIDTH : (member + 1) * WIDTH, :, :],
+                )
+
+        for piece in range(SET_PAIRS):
+            transpose_x(0, piece)
+        for piece in range(SET_PAIRS):
+            regroup_x(0, piece)
+        for piece in range(SET_PAIRS):
+            quantise_x(0, piece)
+        project_o(0)
+        for piece in range(SET_PAIRS):
+            transpose_x(1, piece)
+        for piece in range(SET_PAIRS):
+            regroup_x(1, piece)
+            transpose_x(2, piece)
+        for piece in range(SET_PAIRS):
+            quantise_x(1, piece)
+        for s in range(BATCH + max(LAG, 5) + 1):
+            project_rel(s - LAG)
+            t_statistics(s - 1)
+            for piece in range(SET_PAIRS):
+                regroup_x(s + 2, piece)
+                transpose_x(s + 3, piece)
+            tanh_of_z(s)
+            project_o(s + 1)
+            squares_of_tanh(s)
+            average_over_partitions(s)
+            tanh_of_u(s - 3)
+            row_max(s - LAG)
+            row_exp_sum(s - LAG)
+            u_statistics(s - 4)
+            store_mass(s - LAG)
+            standardise_t(s - 2)
+            for piece in range(SET_PAIRS):
+                quantise_x(s + 2, piece)
+            second_product(s - 2)
+            store_proj(s - 5)

@@ -58,15 +58,19 @@ def tile_selfprojectiondev_pa_e_kernel(
         work = stack.enter_context(tc.tile_pool(name="work", bufs=4))
         small = stack.enter_context(tc.tile_pool(name="small", bufs=4))
         group_pool = stack.enter_context(tc.tile_pool(name="group_pool", bufs=2))
-        psum_flip = stack.enter_context(tc.psum_pool(name="psum_flip", bufs=SET_PAIRS))
+        psum_flip = stack.enter_context(tc.psum_pool(name="psum_flip", bufs=2))
         psum_first = stack.enter_context(tc.psum_pool(name="psum_first", bufs=2 * HALVES))
         psum_one = stack.enter_context(tc.psum_pool(name="psum_one", bufs=1))
+        psum_avg = stack.enter_context(tc.psum_pool(name="psum_avg", bufs=1))
 
         identity = const.tile([P, P], F32)
         make_identity(nc, identity[:])
         averager = const.tile([P, P], F32)
-        nc.vector.memset(averager[:], 1.0 / (ROWS * WIDTH))
-        half = const.tile([P, DEPTHS], F32)
+        nc.vector.memset(averager[:], 0.0)
+        for k in range(DEPTHS_PER_HALF):
+            block = slice(k * WIDTH, (k + 1) * WIDTH)
+            nc.vector.memset(averager[block, block], 1.0 / (ROWS * WIDTH))
+        half = const.tile([P, HALVES], F32)
         nc.vector.memset(half[:], 0.5)
 
         planes = const.tile([P, 3, ALL_WIDTH], U8, align_bytes=64)
@@ -97,7 +101,7 @@ def tile_selfprojectiondev_pa_e_kernel(
 
         def load_x(b):
             x_rows[b] = x_pool.tile([P, PACK, COLS], BF16, name="x_rows")
-            by_set = x[b].rearrange("(q a) j -> q a j", a=PACK)
+            by_set = x[b].rearrange("(a q) j -> q a j", a=PACK)
             for piece in range(SET_PAIRS):
                 sets = slice(2 * piece, 2 * piece + 2)
                 nc.sync.dma_start(out=x_rows[b][:, sets, :], in_=by_set[:, sets, :])
@@ -127,7 +131,7 @@ def tile_selfprojectiondev_pa_e_kernel(
             if not exists(b):
                 return
             words = x_rows[b][:].rearrange("q a j -> q (a j)").bitcast(F32)
-            flipped[(b, piece)] = psum_flip.tile([P, 2, PIECE], F32, name="flipped")
+            flipped[(b, piece)] = psum_flip.tile([P, 2, PIECE], F32, name="flipped", tag="flip")
             for a2 in range(2):
                 a = 2 * piece + a2
                 for u in range(2):
@@ -165,54 +169,40 @@ def tile_selfprojectiondev_pa_e_kernel(
         z = {}
         r = {}
 
-        def project_o(b):
-            if not exists(b):
-                return
-            for h in range(HALVES):
-                z[(b, h)] = psum_first.tile([P, PACK, P], F32, name="z", tag="first")
-            for a in range(PACK):
-                row_set = slice(a * P, (a + 1) * P)
-                for h in range(HALVES):
-                    cols = slice(h * P, (h + 1) * P)
-                    nc.tensor.matmul_mx(
-                        out=z[(b, h)][:, a, :],
-                        lhsT=x_codes[b][:, row_set].bitcast(FP8X4),
-                        lhsT_scale=x_scales[b][:, row_set],
-                        rhs=o_codes[:, cols].bitcast(FP8X4),
-                        rhs_scale=o_plane[:, cols],
-                        start=True,
-                        stop=True,
-                    )
-
-        def project_rel(b):
+        def project(b, product, name, codes, plane):
             if not exists(b):
                 return
             for h in range(HALVES):
                 cols = slice(h * P, (h + 1) * P)
-                r[(b, h)] = psum_first.tile([P, ROWS], F32, name="r", tag="first")
+                product[(b, h)] = psum_first.tile([P, ROWS], F32, name=name, tag="first")
                 nc.tensor.matmul_mx(
-                    out=r[(b, h)][:],
-                    lhsT=rel_codes[:, cols].bitcast(FP8X4),
-                    lhsT_scale=rel_plane[:, cols],
+                    out=product[(b, h)][:],
+                    lhsT=codes[:, cols].bitcast(FP8X4),
+                    lhsT_scale=plane[:, cols],
                     rhs=x_codes[b][:].bitcast(FP8X4),
                     rhs_scale=x_scales[b][:],
                     start=True,
                     stop=True,
                 )
 
+        def project_o(b):
+            project(b, z, "z", o_codes, o_plane)
+
+        def project_rel(b):
+            project(b, r, "r", rel_codes, rel_plane)
+
         neg_max = const.tile([P, QUADRANT], F32, align_bytes=64)
         nc.vector.memset(neg_max[:], 0.0)
         exp_sum = const.tile([P, QUADRANT], F32, align_bytes=64)
         nc.vector.memset(exp_sum[:], 1.0)
 
-        def row_max(b):
+        def row_max(b, h):
             if not exists(b):
                 return
-            for h in range(HALVES):
-                c = HALVES * b + h
-                nc.vector.tensor_reduce(
-                    out=neg_max[:, c : c + 1], in_=r[(b, h)][:], axis=AXIS.X, op=ALU.max, negate=True
-                )
+            c = HALVES * b + h
+            nc.vector.tensor_reduce(
+                out=neg_max[:, c : c + 1], in_=r[(b, h)][:], axis=AXIS.X, op=ALU.max, negate=True
+            )
 
         def row_exp_sum(b):
             if not exists(b):
@@ -273,50 +263,78 @@ def tile_selfprojectiondev_pa_e_kernel(
         averages = {}
         t_moments = {}
         t_std = {}
+        t_turned = {}
         t_grouped = {}
 
         def tanh_of_z(b):
             if not exists(b):
                 return
-            tanh_z[b] = work.tile([P, DEPTHS, WIDTH * PACK], F32, name="tanh_z")
-            sums[b] = small.tile([P, 2 * DEPTHS], F32, name="sums")
-            for d in range(DEPTHS):
-                h, k = divmod(d, DEPTHS_PER_HALF)
+            tanh_z[b] = work.tile([P, HALVES, ROWS], F32, name="tanh_z")
+            sums[b] = small.tile([P, 2 * HALVES], F32, name="sums")
+            for h in range(HALVES):
                 nc.scalar.activation(
-                    out=tanh_z[b][:, d, :].rearrange("q (w a) -> q w a", a=PACK),
-                    in_=z[(b, h)][:, :, k * WIDTH : (k + 1) * WIDTH].rearrange("q a w -> q w a"),
-                    func=ACT.Tanh,
-                    accum_out=sums[b][:, d : d + 1],
+                    out=tanh_z[b][:, h, :], in_=z[(b, h)][:], func=ACT.Tanh, accum_out=sums[b][:, h : h + 1]
                 )
 
         def squares_of_tanh(b):
             if not exists(b):
                 return
-            for d in range(DEPTHS):
-                unread = work.tile([P, WIDTH * PACK], BF16, name="unread_square")
+            for h in range(HALVES):
+                unread = work.tile([P, ROWS], BF16, name="unread_square")
                 nc.scalar.activation(
                     out=unread[:],
-                    in_=tanh_z[b][:, d, :],
+                    in_=tanh_z[b][:, h, :],
                     func=ACT.Square,
-                    accum_out=sums[b][:, DEPTHS + d : DEPTHS + d + 1],
+                    accum_out=sums[b][:, HALVES + h : HALVES + h + 1],
                 )
 
-        def average_over_partitions(b):
+        def average_over_matrices(b):
             if not exists(b):
                 return
-            averages[b] = psum_one.tile([P, 2 * DEPTHS], F32, name="averages")
+            averages[b] = psum_avg.tile([P, 2 * HALVES], F32, name="averages")
             nc.tensor.matmul(out=averages[b][:], lhsT=averager[:], rhs=sums[b][:], start=True, stop=True)
 
         def t_statistics(b):
             if not exists(b):
                 return
-            t_moments[b] = small.tile([P, 2 * DEPTHS], F32, name="t_moments")
+            t_moments[b] = small.tile([P, 2 * HALVES], F32, name="t_moments")
             nc.vector.tensor_copy(out=t_moments[b][:], in_=averages[b][:])
             t_std[b] = std_plus_eps(
-                t_moments[b][:, 0:DEPTHS], t_moments[b][:, DEPTHS : 2 * DEPTHS], ROWS * WIDTH
+                t_moments[b][:, 0:HALVES], t_moments[b][:, HALVES : 2 * HALVES], ROWS * WIDTH
             )
 
+        t_rows = {}
+
         def standardise_t(b):
+            if not exists(b):
+                return
+            inv = small.tile([P, HALVES], F32, name="t_inv")
+            nc.vector.reciprocal(out=inv[:], in_=t_std[b][:])
+            t_rows[b] = work.tile([P, HALVES, ROWS], BF16, name="t_rows")
+            for h in range(HALVES):
+                nc.vector.tensor_scalar(
+                    out=t_rows[b][:, h, :],
+                    in0=tanh_z[b][:, h, :],
+                    scalar1=t_moments[b][:, h : h + 1],
+                    scalar2=inv[:, h : h + 1],
+                    op0=ALU.subtract,
+                    op1=ALU.mult,
+                )
+
+        def transpose_t(b):
+            if not exists(b):
+                return
+            t_turned[b] = psum_flip.tile([P, 2, ALL_WIDTH], F32, name="t_turned", tag="flip")
+            words = t_rows[b][:].rearrange("c h i -> c (h i)").bitcast(F32)
+            for h in range(HALVES):
+                for u in range(2):
+                    nc.tensor.transpose(
+                        t_turned[b][:, u, h * P : (h + 1) * P],
+                        words[:, h * ROWS // 2 + u : (h + 1) * ROWS // 2 : 2],
+                        identity[:],
+                    )
+
+        def regroup_t(b):
             if not exists(b):
                 return
             group, member = divmod(b, GROUP)
@@ -324,17 +342,13 @@ def tile_selfprojectiondev_pa_e_kernel(
                 t_grouped[group] = group_pool.tile(
                     [P, DEPTHS, GROUP, WIDTH * PACK], BF16, name="t_grouped", align_bytes=64
                 )
-            inv = small.tile([P, DEPTHS], F32, name="t_inv")
-            nc.vector.reciprocal(out=inv[:], in_=t_std[b][:])
-            for d in range(DEPTHS):
-                nc.vector.tensor_scalar(
-                    out=t_grouped[group][:, d, member, :],
-                    in0=tanh_z[b][:, d, :],
-                    scalar1=t_moments[b][:, d : d + 1],
-                    scalar2=inv[:, d : d + 1],
-                    op0=ALU.subtract,
-                    op1=ALU.mult,
-                )
+            out = (
+                t_grouped[group][:]
+                .rearrange("q d m e -> q (d m e)")
+                .bitcast(F32)
+                .rearrange("q (d m w u) -> q d m w u", d=DEPTHS, m=GROUP, u=2)[:, :, member, :, :]
+            )
+            nc.scalar.copy(out=out, in_=t_turned[b][:].rearrange("q u (d w) -> q d w u", d=DEPTHS))
 
         u = {}
         tanh_u = {}
@@ -445,26 +459,30 @@ def tile_selfprojectiondev_pa_e_kernel(
             transpose_x(1, piece)
         for piece in range(SET_PAIRS):
             regroup_x(1, piece)
-            transpose_x(2, piece)
+        transpose_x(2, 0)
         for piece in range(SET_PAIRS):
             quantise_x(1, piece)
         for s in range(BATCH + max(LAG, 5) + 1):
-            project_rel(s - LAG)
             t_statistics(s - 1)
-            for piece in range(SET_PAIRS):
-                regroup_x(s + 2, piece)
-                transpose_x(s + 3, piece)
+            transpose_x(s + 2, 1)
+            project_rel(s - LAG)
+            regroup_x(s + 2, 0)
             tanh_of_z(s)
             project_o(s + 1)
+            second_product(s - 2)
+            row_max(s - LAG, 0)
+            regroup_x(s + 2, 1)
+            row_max(s - LAG, 1)
             squares_of_tanh(s)
-            average_over_partitions(s)
-            tanh_of_u(s - 3)
-            row_max(s - LAG)
+            average_over_matrices(s)
+            standardise_t(s - 1)
+            transpose_t(s - 1)
+            transpose_x(s + 3, 0)
             row_exp_sum(s - LAG)
-            u_statistics(s - 4)
             store_mass(s - LAG)
-            standardise_t(s - 2)
+            regroup_t(s - 1)
+            tanh_of_u(s - 2)
             for piece in range(SET_PAIRS):
                 quantise_x(s + 2, piece)
-            second_product(s - 2)
-            store_proj(s - 5)
+            u_statistics(s - 3)
+            store_proj(s - 4)

@@ -28,8 +28,7 @@ ALL_WIDTH = DEPTHS * WIDTH
 HALVES = ALL_WIDTH // P
 DEPTHS_PER_HALF = DEPTHS // HALVES
 WORDS = COLS // 2
-GROUP = P // WIDTH
-PAIR_WIDTH = 2 * WIDTH
+GROUP = 2
 SET_PAIRS = PACK // 2
 PIECE = ROWS // SET_PAIRS
 
@@ -57,11 +56,12 @@ def tile_selfprojectiondev_pa_e_kernel(
         x_pool = stack.enter_context(tc.tile_pool(name="x_pool", bufs=BATCH))
         work = stack.enter_context(tc.tile_pool(name="work", bufs=4))
         small = stack.enter_context(tc.tile_pool(name="small", bufs=4))
-        group_pool = stack.enter_context(tc.tile_pool(name="group_pool", bufs=2))
+        group_pool = stack.enter_context(tc.tile_pool(name="group_pool", bufs=BATCH // GROUP))
         psum_flip = stack.enter_context(tc.psum_pool(name="psum_flip", bufs=2))
-        psum_first = stack.enter_context(tc.psum_pool(name="psum_first", bufs=2 * HALVES))
-        psum_one = stack.enter_context(tc.psum_pool(name="psum_one", bufs=1))
+        psum_first = stack.enter_context(tc.psum_pool(name="psum_first", bufs=3))
+        psum_t = stack.enter_context(tc.psum_pool(name="psum_t", bufs=1))
         psum_avg = stack.enter_context(tc.psum_pool(name="psum_avg", bufs=1))
+        psum_u = stack.enter_context(tc.psum_pool(name="psum_u", bufs=1))
 
         identity = const.tile([P, P], F32)
         make_identity(nc, identity[:])
@@ -70,7 +70,7 @@ def tile_selfprojectiondev_pa_e_kernel(
         for k in range(DEPTHS_PER_HALF):
             block = slice(k * WIDTH, (k + 1) * WIDTH)
             nc.vector.memset(averager[block, block], 1.0 / (ROWS * WIDTH))
-        half = const.tile([P, HALVES], F32)
+        half = const.tile([P, GROUP * HALVES], F32)
         nc.vector.memset(half[:], 0.5)
 
         planes = const.tile([P, 3, ALL_WIDTH], U8, align_bytes=64)
@@ -141,11 +141,11 @@ def tile_selfprojectiondev_pa_e_kernel(
                         identity[:],
                     )
 
-        def regroup_x(b, piece):
+        def regroup_x(b, piece, copy=nc.vector.tensor_copy):
             if not exists(b):
                 return
             x_grouped[(b, piece)] = work.tile([P, PIECE, PACK], BF16, name="x_grouped", align_bytes=64)
-            nc.vector.tensor_copy(
+            copy(
                 out=x_grouped[(b, piece)][:]
                 .rearrange("k c t -> k (c t)")
                 .bitcast(F32)
@@ -169,12 +169,12 @@ def tile_selfprojectiondev_pa_e_kernel(
         z = {}
         r = {}
 
-        def project(b, product, name, codes, plane):
+        def project(b, product, name, pool, tag, codes, plane):
             if not exists(b):
                 return
             for h in range(HALVES):
                 cols = slice(h * P, (h + 1) * P)
-                product[(b, h)] = psum_first.tile([P, ROWS], F32, name=name, tag="first")
+                product[(b, h)] = pool.tile([P, ROWS], F32, name=name, tag=tag)
                 nc.tensor.matmul_mx(
                     out=product[(b, h)][:],
                     lhsT=codes[:, cols].bitcast(FP8X4),
@@ -186,10 +186,13 @@ def tile_selfprojectiondev_pa_e_kernel(
                 )
 
         def project_o(b):
-            project(b, z, "z", o_codes, o_plane)
+            project(b, z, "z", psum_first, "first", o_codes, o_plane)
 
         def project_rel(b):
-            project(b, r, "r", rel_codes, rel_plane)
+            if b % 2 == 0:
+                project(b, r, "r", psum_flip, "flip", rel_codes, rel_plane)
+            else:
+                project(b, r, "r", psum_first, "first", rel_codes, rel_plane)
 
         neg_max = const.tile([P, QUADRANT], F32, align_bytes=64)
         nc.vector.memset(neg_max[:], 0.0)
@@ -291,7 +294,7 @@ def tile_selfprojectiondev_pa_e_kernel(
         def average_over_matrices(b):
             if not exists(b):
                 return
-            averages[b] = psum_avg.tile([P, 2 * HALVES], F32, name="averages")
+            averages[b] = psum_avg.tile([P, 2 * HALVES], F32, name="averages", tag="avg")
             nc.tensor.matmul(out=averages[b][:], lhsT=averager[:], rhs=sums[b][:], start=True, stop=True)
 
         def t_statistics(b):
@@ -303,20 +306,25 @@ def tile_selfprojectiondev_pa_e_kernel(
                 t_moments[b][:, 0:HALVES], t_moments[b][:, HALVES : 2 * HALVES], ROWS * WIDTH
             )
 
+        t_inv = {}
         t_rows = {}
+
+        def invert_t_std(b):
+            if not exists(b):
+                return
+            t_inv[b] = small.tile([P, HALVES], F32, name="t_inv")
+            nc.vector.reciprocal(out=t_inv[b][:], in_=t_std[b][:])
 
         def standardise_t(b):
             if not exists(b):
                 return
-            inv = small.tile([P, HALVES], F32, name="t_inv")
-            nc.vector.reciprocal(out=inv[:], in_=t_std[b][:])
             t_rows[b] = work.tile([P, HALVES, ROWS], BF16, name="t_rows")
             for h in range(HALVES):
                 nc.vector.tensor_scalar(
                     out=t_rows[b][:, h, :],
                     in0=tanh_z[b][:, h, :],
                     scalar1=t_moments[b][:, h : h + 1],
-                    scalar2=inv[:, h : h + 1],
+                    scalar2=t_inv[b][:, h : h + 1],
                     op0=ALU.subtract,
                     op1=ALU.mult,
                 )
@@ -324,7 +332,7 @@ def tile_selfprojectiondev_pa_e_kernel(
         def transpose_t(b):
             if not exists(b):
                 return
-            t_turned[b] = psum_flip.tile([P, 2, ALL_WIDTH], F32, name="t_turned", tag="flip")
+            t_turned[b] = psum_t.tile([P, 2, ALL_WIDTH], F32, name="t_turned", tag="t")
             words = t_rows[b][:].rearrange("c h i -> c (h i)").bitcast(F32)
             for h in range(HALVES):
                 for u in range(2):
@@ -334,59 +342,57 @@ def tile_selfprojectiondev_pa_e_kernel(
                         identity[:],
                     )
 
-        def regroup_t(b):
+        def regroup_t(b, copy=nc.scalar.copy):
             if not exists(b):
                 return
-            group, member = divmod(b, GROUP)
-            if member == 0:
-                t_grouped[group] = group_pool.tile(
-                    [P, DEPTHS, GROUP, WIDTH * PACK], BF16, name="t_grouped", align_bytes=64
-                )
-            out = (
-                t_grouped[group][:]
-                .rearrange("q d m e -> q (d m e)")
+            t_grouped[b] = work.tile([P, ALL_WIDTH, PACK], BF16, name="t_grouped", align_bytes=64)
+            copy(
+                out=t_grouped[b][:]
+                .rearrange("q c a -> q (c a)")
                 .bitcast(F32)
-                .rearrange("q (d m w u) -> q d m w u", d=DEPTHS, m=GROUP, u=2)[:, :, member, :, :]
+                .rearrange("q (c u) -> q c u", u=2),
+                in_=t_turned[b][:].rearrange("q u c -> q c u"),
             )
-            nc.scalar.copy(out=out, in_=t_turned[b][:].rearrange("q u (d w) -> q d w u", d=DEPTHS))
 
+        t_codes = {}
+        t_scales = {}
         u = {}
         tanh_u = {}
-        squares_u = {}
-        centred_u = {}
+        u_sums = {}
+        u_averages = {}
+        u_moments = {}
         u_std = {}
-        u_row_sums = {}
-        for moment in range(2):
-            u_row_sums[moment] = const.tile([P, QUADRANT], F32, name="u_row_sums%d" % moment, align_bytes=64)
-            nc.vector.memset(u_row_sums[moment][:], 0.0)
+        u_inv = {}
+        centred_u = {}
 
         def closes_group(b):
             return exists(b) and b % GROUP == GROUP - 1
 
-        def second_product(b):
-            if not closes_group(b):
+        def quantise_t(b):
+            if not exists(b):
                 return
-            group = b // GROUP
-            t_codes = group_pool.tile([P, DEPTHS * P], U32, name="t_codes", align_bytes=64)
-            t_scales = group_pool.tile([P, DEPTHS * P], U8, name="t_scales", align_bytes=64)
-            u[group] = psum_one.tile([P, DEPTHS, PAIR_WIDTH], F32, name="u")
+            t_codes[b] = work.tile([P, ALL_WIDTH], U32, name="t_codes", align_bytes=64)
+            t_scales[b] = work.tile([P, ALL_WIDTH], U8, name="t_scales", align_bytes=64)
+            nc.vector.quantize_mx(
+                out=t_codes[b][:].bitcast(FP8X4),
+                scales=t_scales[b][:],
+                in_=t_grouped[b][:].rearrange("q c a -> q (c a)"),
+            )
+
+        def second_product(b):
+            if not exists(b):
+                return
+            group, member = divmod(b, GROUP)
+            if member == 0:
+                u[group] = psum_u.tile([P, GROUP, HALVES, P], F32, name="u", tag="u")
             for h in range(HALVES):
-                depths = slice(h * DEPTHS_PER_HALF, (h + 1) * DEPTHS_PER_HALF)
-                cols = slice(h * DEPTHS_PER_HALF * P, (h + 1) * DEPTHS_PER_HALF * P)
-                nc.vector.quantize_mx(
-                    out=t_codes[:, cols].bitcast(FP8X4),
-                    scales=t_scales[:, cols],
-                    in_=t_grouped[group][:, depths, :, :].rearrange("q d m e -> q (d m e)"),
-                )
-            for d in range(DEPTHS):
-                members = slice(d * P, (d + 1) * P)
-                pair = slice((d // 2) * PAIR_WIDTH, (d // 2 + 1) * PAIR_WIDTH)
+                cols = slice(h * P, (h + 1) * P)
                 nc.tensor.matmul_mx(
-                    out=u[group][:, d, :],
-                    lhsT=t_codes[:, members].bitcast(FP8X4),
-                    lhsT_scale=t_scales[:, members],
-                    rhs=p_codes[:, pair].bitcast(FP8X4),
-                    rhs_scale=p_plane[:, pair],
+                    out=u[group][:, member, h, :],
+                    lhsT=t_codes[b][:, cols].bitcast(FP8X4),
+                    lhsT_scale=t_scales[b][:, cols],
+                    rhs=p_codes[:, cols].bitcast(FP8X4),
+                    rhs_scale=p_plane[:, cols],
                     start=True,
                     stop=True,
                 )
@@ -395,94 +401,206 @@ def tile_selfprojectiondev_pa_e_kernel(
             if not closes_group(b):
                 return
             group = b // GROUP
-            own = u[group][:].rearrange("q (e f) (g v) -> q e (f g) v", f=2, g=2)[:, :, 0:4:3, :]
-            tanh_u[group] = group_pool.tile([P, DEPTHS, WIDTH], F32, name="tanh_u")
-            nc.scalar.activation(
-                out=tanh_u[group][:].rearrange("q (e f) v -> q e f v", f=2), in_=own, func=ACT.Tanh
-            )
-            squares_u[group] = group_pool.tile([P, DEPTHS, WIDTH], F32, name="squares_u")
+            tanh_u[group] = group_pool.tile([P, GROUP * HALVES, WIDTH], F32, name="tanh_u")
+            by_pass = u[group][:].rearrange("c m h e -> c (m h) e")
+            for k in range(DEPTHS_PER_HALF):
+                own = slice(k * WIDTH, (k + 1) * WIDTH)
+                nc.scalar.activation(out=tanh_u[group][own, :, :], in_=by_pass[own, :, own], func=ACT.Tanh)
+
+        squares_u = {}
+
+        def squares_of_u(b):
+            if not closes_group(b):
+                return
+            group = b // GROUP
+            squares_u[group] = group_pool.tile([P, GROUP * HALVES, WIDTH], F32, name="squares_u")
             nc.scalar.activation(out=squares_u[group][:], in_=tanh_u[group][:], func=ACT.Square)
 
-        def spread_over_member(column):
-            repeated = small.tile([P, QUADRANT], F32, name="repeated", align_bytes=64)
-            nc.vector.tensor_copy(out=repeated[:], in_=column[:].to_broadcast([P, QUADRANT]))
-            spread = small.tile([P, QUADRANT], F32, name="spread", align_bytes=64)
-            nc.vector.transpose(out=spread[:], in_=repeated[:])
-            return spread[:, 0:DEPTHS].unsqueeze(2).to_broadcast([P, DEPTHS, WIDTH])
+        def sum_u(b):
+            if not closes_group(b):
+                return
+            group = b // GROUP
+            u_sums[group] = small.tile([P, 2, GROUP * HALVES], F32, name="u_sums")
+            nc.vector.reduce_sum(out=u_sums[group][:, 0, :], in_=tanh_u[group][:], axis=AXIS.X)
+
+        def sum_squares_of_u(b):
+            if not closes_group(b):
+                return
+            group = b // GROUP
+            nc.vector.reduce_sum(out=u_sums[group][:, 1, :], in_=squares_u[group][:], axis=AXIS.X)
+
+        def average_u(b):
+            if not closes_group(b):
+                return
+            group = b // GROUP
+            u_averages[group] = psum_avg.tile([P, 2, GROUP * HALVES], F32, name="u_averages", tag="avg")
+            nc.tensor.matmul(
+                out=u_averages[group][:].rearrange("c k n -> c (k n)"),
+                lhsT=averager[:],
+                rhs=u_sums[group][:].rearrange("c k n -> c (k n)"),
+                start=True,
+                stop=True,
+            )
 
         def u_statistics(b):
             if not closes_group(b):
                 return
             group = b // GROUP
-            by_depth = {}
-            moments = {}
-            for moment, values in enumerate((tanh_u[group], squares_u[group])):
-                nc.vector.reduce_sum(out=u_row_sums[moment][:, 0:DEPTHS], in_=values[:], axis=AXIS.X)
-            for moment in range(2):
-                by_depth[moment] = small.tile([P, QUADRANT], F32, name="by_depth", align_bytes=64)
-                nc.vector.transpose(out=by_depth[moment][:], in_=u_row_sums[moment][:])
-            for moment in range(2):
-                moments[moment] = small.tile([P, 1], F32, name="u_moment")
-                nc.vector.tensor_scalar(
-                    out=by_depth[moment][:], in0=by_depth[moment][:],
-                    scalar1=1.0 / (WIDTH * WIDTH), scalar2=None, op0=ALU.mult, op1=ALU.add,
-                    accum_out=moments[moment][:],
-                )
-            u_std[group] = std_plus_eps(moments[0][:], moments[1][:], WIDTH * WIDTH)
-            centred_u[group] = group_pool.tile([P, DEPTHS, WIDTH], F32, name="centred_u")
-            nc.vector.tensor_sub(
-                out=centred_u[group][:], in0=tanh_u[group][:], in1=spread_over_member(moments[0])
+            u_moments[group] = small.tile([P, 2, GROUP * HALVES], F32, name="u_moments")
+            nc.vector.tensor_scalar_mul(
+                out=u_moments[group][:], in0=u_averages[group][:], scalar1=float(ROWS // WIDTH)
             )
+            u_std[group] = std_plus_eps(
+                u_moments[group][:, 0, :], u_moments[group][:, 1, :], WIDTH * WIDTH
+            )
+
+        def each_entry(columns):
+            return columns.unsqueeze(2).to_broadcast([P, GROUP * HALVES, WIDTH])
+
+        def centre_u(b):
+            if not closes_group(b):
+                return
+            group = b // GROUP
+            centred_u[group] = group_pool.tile([P, GROUP * HALVES, WIDTH], F32, name="centred_u")
+            nc.vector.tensor_sub(
+                out=centred_u[group][:], in0=tanh_u[group][:], in1=each_entry(u_moments[group][:, 0, :])
+            )
+
+        def invert_u_std(b):
+            if not closes_group(b):
+                return
+            group = b // GROUP
+            u_inv[group] = small.tile([P, GROUP * HALVES], F32, name="u_inv")
+            nc.vector.reciprocal(out=u_inv[group][:], in_=u_std[group][:])
 
         def store_proj(b):
             if not closes_group(b):
                 return
             group = b // GROUP
-            inv = small.tile([P, 1], F32, name="u_inv")
-            nc.vector.reciprocal(out=inv[:], in_=u_std[group][:])
-            proj = group_pool.tile([P, DEPTHS, WIDTH], F32, name="proj")
-            nc.vector.tensor_mul(out=proj[:], in0=centred_u[group][:], in1=spread_over_member(inv))
-            for member in range(GROUP):
-                nc.sync.dma_start(
-                    out=out_0[group * GROUP + member].rearrange("d w v -> w d v"),
-                    in_=proj[member * WIDTH : (member + 1) * WIDTH, :, :],
-                )
+            proj = group_pool.tile([P, GROUP * HALVES, WIDTH], F32, name="proj")
+            nc.vector.tensor_mul(out=proj[:], in0=centred_u[group][:], in1=each_entry(u_inv[group][:]))
+            members = slice(group * GROUP, (group + 1) * GROUP)
+            nc.sync.dma_start(
+                out=out_0[members].rearrange("m (h k) w v -> (k w) (m h) v", h=HALVES), in_=proj[:]
+            )
 
         for piece in range(SET_PAIRS):
             transpose_x(0, piece)
-        for piece in range(SET_PAIRS):
-            regroup_x(0, piece)
-        for piece in range(SET_PAIRS):
-            quantise_x(0, piece)
-        project_o(0)
+        regroup_x(0, 0)
+        regroup_x(0, 1, nc.scalar.copy)
+        quantise_x(0, 0)
+        quantise_x(0, 1)
         for piece in range(SET_PAIRS):
             transpose_x(1, piece)
+        project_o(0)
         for piece in range(SET_PAIRS):
             regroup_x(1, piece)
-        transpose_x(2, 0)
+            transpose_x(2, piece)
         for piece in range(SET_PAIRS):
             quantise_x(1, piece)
-        for s in range(BATCH + max(LAG, 5) + 1):
-            t_statistics(s - 1)
-            transpose_x(s + 2, 1)
-            project_rel(s - LAG)
+        for s in range(BATCH):
             regroup_x(s + 2, 0)
-            tanh_of_z(s)
-            project_o(s + 1)
-            second_product(s - 2)
-            row_max(s - LAG, 0)
-            regroup_x(s + 2, 1)
-            row_max(s - LAG, 1)
-            squares_of_tanh(s)
-            average_over_matrices(s)
-            standardise_t(s - 1)
-            transpose_t(s - 1)
+            t_statistics(s - 1)
             transpose_x(s + 3, 0)
-            row_exp_sum(s - LAG)
-            store_mass(s - LAG)
-            regroup_t(s - 1)
-            tanh_of_u(s - 2)
+            regroup_x(s + 2, 1)
+            transpose_x(s + 3, 1)
+            invert_t_std(s - 2)
             for piece in range(SET_PAIRS):
                 quantise_x(s + 2, piece)
-            u_statistics(s - 3)
-            store_proj(s - 4)
+            quantise_t(s - 4)
+            tanh_of_z(s)
+            if s - 3 < 4:
+                regroup_t(s - 3)
+            project_o(s + 1)
+            second_product(s - 4)
+            project_rel(s - 6)
+            standardise_t(s - 2)
+            transpose_t(s - 2)
+            sum_u(s - 5)
+            sum_squares_of_u(s - 5)
+            average_u(s - 5)
+            row_max(s - 6, 0)
+            u_statistics(s - 5)
+            row_max(s - 6, 1)
+            centre_u(s - 5)
+            if s - 2 >= 4:
+                regroup_t(s - 2, nc.vector.tensor_copy)
+            squares_of_tanh(s)
+            average_over_matrices(s)
+            tanh_of_u(s - 4)
+            row_exp_sum(s - 6)
+            squares_of_u(s - 4)
+            invert_u_std(s - 6)
+            store_proj(s - 6)
+        invert_t_std(6)
+        project_rel(2)
+        quantise_t(4)
+        t_statistics(7)
+        standardise_t(6)
+        transpose_t(6)
+        second_product(4)
+        quantise_t(5)
+        second_product(5)
+        project_rel(3)
+        row_max(2, 0)
+        row_max(2, 1)
+        regroup_t(6)
+        row_exp_sum(2)
+        store_mass(2)
+        row_max(3, 0)
+        tanh_of_u(5)
+        squares_of_u(5)
+        project_rel(4)
+        sum_u(3)
+        sum_squares_of_u(3)
+        average_u(3)
+        invert_t_std(7)
+        quantise_t(6)
+        second_product(6)
+        standardise_t(7)
+        transpose_t(7)
+        u_statistics(3)
+        centre_u(3)
+        row_max(3, 1)
+        sum_u(5)
+        sum_squares_of_u(5)
+        average_u(5)
+        row_exp_sum(3)
+        store_mass(3)
+        row_max(4, 0)
+        project_rel(5)
+        regroup_t(7)
+        u_statistics(5)
+        centre_u(5)
+        row_max(4, 1)
+        row_exp_sum(4)
+        store_mass(4)
+        quantise_t(7)
+        second_product(7)
+        project_rel(6)
+        row_max(5, 0)
+        row_max(5, 1)
+        tanh_of_u(7)
+        squares_of_u(7)
+        invert_u_std(3)
+        store_proj(3)
+        row_exp_sum(5)
+        store_mass(5)
+        row_max(6, 0)
+        project_rel(7)
+        sum_u(7)
+        sum_squares_of_u(7)
+        average_u(7)
+        row_max(6, 1)
+        u_statistics(7)
+        centre_u(7)
+        row_exp_sum(6)
+        store_mass(6)
+        row_max(7, 0)
+        row_max(7, 1)
+        invert_u_std(5)
+        store_proj(5)
+        row_exp_sum(7)
+        store_mass(7)
+        invert_u_std(7)
+        store_proj(7)

@@ -1,3 +1,4 @@
+import math
 from contextlib import ExitStack
 
 import concourse.mybir as mybir
@@ -28,7 +29,7 @@ ALL_WIDTH = DEPTHS * WIDTH
 HALVES = ALL_WIDTH // P
 DEPTHS_PER_HALF = DEPTHS // HALVES
 WORDS = COLS // 2
-GROUP = 2
+GROUPS = ((0, 1), (2, 3), (4, 5), (6, 7))
 SET_PAIRS = PACK // 2
 PIECE = ROWS // SET_PAIRS
 
@@ -55,11 +56,11 @@ def tile_selfprojectiondev_pa_e_kernel(
         const = stack.enter_context(tc.tile_pool(name="const", bufs=1))
         x_pool = stack.enter_context(tc.tile_pool(name="x_pool", bufs=BATCH))
         work = stack.enter_context(tc.tile_pool(name="work", bufs=4))
-        small = stack.enter_context(tc.tile_pool(name="small", bufs=4))
-        group_pool = stack.enter_context(tc.tile_pool(name="group_pool", bufs=BATCH // GROUP))
+        tanh_pool = stack.enter_context(tc.tile_pool(name="tanh_pool", bufs=BATCH))
+        small = stack.enter_context(tc.tile_pool(name="small", bufs=2 * len(GROUPS)))
+        group_pool = stack.enter_context(tc.tile_pool(name="group_pool", bufs=len(GROUPS)))
         psum_flip = stack.enter_context(tc.psum_pool(name="psum_flip", bufs=2))
-        psum_first = stack.enter_context(tc.psum_pool(name="psum_first", bufs=3))
-        psum_t = stack.enter_context(tc.psum_pool(name="psum_t", bufs=1))
+        psum_first = stack.enter_context(tc.psum_pool(name="psum_first", bufs=4))
         psum_avg = stack.enter_context(tc.psum_pool(name="psum_avg", bufs=1))
         psum_u = stack.enter_context(tc.psum_pool(name="psum_u", bufs=1))
 
@@ -69,8 +70,8 @@ def tile_selfprojectiondev_pa_e_kernel(
         nc.vector.memset(averager[:], 0.0)
         for k in range(DEPTHS_PER_HALF):
             block = slice(k * WIDTH, (k + 1) * WIDTH)
-            nc.vector.memset(averager[block, block], 1.0 / (ROWS * WIDTH))
-        half = const.tile([P, GROUP * HALVES], F32)
+            nc.vector.memset(averager[block, block], 1.0 / (WIDTH * WIDTH))
+        half = const.tile([P, 2 * HALVES], F32)
         nc.vector.memset(half[:], 0.5)
 
         planes = const.tile([P, 3, ALL_WIDTH], U8, align_bytes=64)
@@ -119,17 +120,12 @@ def tile_selfprojectiondev_pa_e_kernel(
         for b in range(4, BATCH):
             load_x(b)
 
-        def exists(b):
-            return 0 <= b < BATCH
-
         flipped = {}
         x_grouped = {}
         x_codes = {}
         x_scales = {}
 
         def transpose_x(b, piece):
-            if not exists(b):
-                return
             words = x_rows[b][:].rearrange("q a j -> q (a j)").bitcast(F32)
             flipped[(b, piece)] = psum_flip.tile([P, 2, PIECE], F32, name="flipped", tag="flip")
             for a2 in range(2):
@@ -142,8 +138,6 @@ def tile_selfprojectiondev_pa_e_kernel(
                     )
 
         def regroup_x(b, piece, copy=nc.vector.tensor_copy):
-            if not exists(b):
-                return
             x_grouped[(b, piece)] = work.tile([P, PIECE, PACK], BF16, name="x_grouped", align_bytes=64)
             copy(
                 out=x_grouped[(b, piece)][:]
@@ -154,8 +148,6 @@ def tile_selfprojectiondev_pa_e_kernel(
             )
 
         def quantise_x(b, piece):
-            if not exists(b):
-                return
             if piece == 0:
                 x_codes[b] = x_pool.tile([P, ROWS], U32, name="x_codes", align_bytes=64)
                 x_scales[b] = x_pool.tile([P, ROWS], U8, name="x_scales", align_bytes=64)
@@ -169,30 +161,24 @@ def tile_selfprojectiondev_pa_e_kernel(
         z = {}
         r = {}
 
-        def project(b, product, name, pool, tag, codes, plane):
-            if not exists(b):
-                return
-            for h in range(HALVES):
-                cols = slice(h * P, (h + 1) * P)
-                product[(b, h)] = pool.tile([P, ROWS], F32, name=name, tag=tag)
-                nc.tensor.matmul_mx(
-                    out=product[(b, h)][:],
-                    lhsT=codes[:, cols].bitcast(FP8X4),
-                    lhsT_scale=plane[:, cols],
-                    rhs=x_codes[b][:].bitcast(FP8X4),
-                    rhs_scale=x_scales[b][:],
-                    start=True,
-                    stop=True,
-                )
+        def project(product, b, h, name, pool, tag, codes, plane):
+            cols = slice(h * P, (h + 1) * P)
+            product[(b, h)] = pool.tile([P, ROWS], F32, name=name, tag=tag)
+            nc.tensor.matmul_mx(
+                out=product[(b, h)][:],
+                lhsT=codes[:, cols].bitcast(FP8X4),
+                lhsT_scale=plane[:, cols],
+                rhs=x_codes[b][:].bitcast(FP8X4),
+                rhs_scale=x_scales[b][:],
+                start=True,
+                stop=True,
+            )
 
-        def project_o(b):
-            project(b, z, "z", psum_first, "first", o_codes, o_plane)
+        def project_o(b, h):
+            project(z, b, h, "z", psum_first, "first", o_codes, o_plane)
 
-        def project_rel(b):
-            if b % 2 == 0:
-                project(b, r, "r", psum_flip, "flip", rel_codes, rel_plane)
-            else:
-                project(b, r, "r", psum_first, "first", rel_codes, rel_plane)
+        def project_rel(b, h):
+            project(r, b, h, "r", psum_first, "first", rel_codes, rel_plane)
 
         neg_max = const.tile([P, QUADRANT], F32, align_bytes=64)
         nc.vector.memset(neg_max[:], 0.0)
@@ -200,38 +186,34 @@ def tile_selfprojectiondev_pa_e_kernel(
         nc.vector.memset(exp_sum[:], 1.0)
 
         def row_max(b, h):
-            if not exists(b):
-                return
             c = HALVES * b + h
             nc.vector.tensor_reduce(
                 out=neg_max[:, c : c + 1], in_=r[(b, h)][:], axis=AXIS.X, op=ALU.max, negate=True
             )
 
-        def row_exp_sum(b):
-            if not exists(b):
-                return
-            for h in range(HALVES):
-                c = HALVES * b + h
-                unread = work.tile([P, ROWS], BF16, name="unread_exp")
-                nc.scalar.activation(
-                    out=unread[:],
-                    in_=r[(b, h)][:],
-                    func=ACT.Exp,
-                    bias=neg_max[:, c : c + 1],
-                    accum_out=exp_sum[:, c : c + 1],
-                )
+        def row_exp_sum(b, h):
+            c = HALVES * b + h
+            unread = work.tile([P, ROWS], BF16, name="unread_exp")
+            nc.scalar.activation(
+                out=unread[:],
+                in_=r[(b, h)][:],
+                func=ACT.Exp,
+                bias=neg_max[:, c : c + 1],
+                accum_out=exp_sum[:, c : c + 1],
+            )
 
-        def store_mass(b):
-            if b != BATCH - 1:
-                return
-            neg_max_t = const.tile([P, QUADRANT], F32, align_bytes=64)
+        neg_max_t = const.tile([P, QUADRANT], F32, align_bytes=64)
+        neg_top = const.tile([P, 1], F32)
+        rescale = const.tile([P, WIDTH], F32)
+
+        def join_maxima():
             nc.vector.transpose(out=neg_max_t[:], in_=neg_max[:])
-            neg_top = const.tile([P, 1], F32)
             nc.vector.tensor_reduce(out=neg_top[:], in_=neg_max_t[:], axis=AXIS.X, op=ALU.min)
-            rescale = const.tile([P, WIDTH], F32)
             nc.scalar.activation(
                 out=rescale[:], in_=neg_max_t[:], func=ACT.Exp, bias=neg_top[:], scale=-1.0
             )
+
+        def store_mass():
             exp_sum_t = const.tile([P, QUADRANT], F32, align_bytes=64)
             nc.vector.transpose(out=exp_sum_t[:], in_=exp_sum[:])
             unnormalised = const.tile([P, WIDTH], F32)
@@ -247,104 +229,126 @@ def tile_selfprojectiondev_pa_e_kernel(
                     out=by_depth[k], in_=mass[QUADRANT * k : QUADRANT * k + HALVES * BATCH, :]
                 )
 
-        def std_plus_eps(mean, mean_of_squares, count):
-            shape = [P, mean.shape[1]]
-            var = small.tile(shape, F32, name="var")
-            nc.gpsimd.tensor_tensor(out=var[:], in0=mean, in1=mean, op=ALU.mult)
-            nc.gpsimd.tensor_tensor(out=var[:], in0=mean_of_squares, in1=var[:], op=ALU.subtract)
-            nc.gpsimd.tensor_scalar(
-                out=var[:], in0=var[:], scalar1=count / (count - 1.0), scalar2=0.0,
-                op0=ALU.mult, op1=ALU.max,
-            )
-            std = small.tile(shape, F32, name="std")
-            nc.gpsimd.tensor_tensor(out=std[:], in0=var[:], in1=half[:, 0 : shape[1]], op=ALU.pow)
-            nc.gpsimd.tensor_scalar_add(out=std[:], in0=std[:], scalar1=EPS)
-            return std
-
-        tanh_z = {}
         sums = {}
         averages = {}
-        t_moments = {}
-        t_std = {}
+        moments = {}
+        mean_squared = {}
+        variance = {}
+        root = {}
+        inverse = {}
+
+        def group_of(b):
+            return [b in group for group in GROUPS].index(True)
+
+        def columns(group):
+            return len(GROUPS[group]) * HALVES
+
+        def new_sums(what, group):
+            sums[what, group] = small.tile([P, 2, columns(group)], F32, name="sums")
+
+        def average(what, group):
+            averages[what, group] = psum_avg.tile([P, 2, columns(group)], F32, name="averages", tag="avg")
+            nc.tensor.matmul(
+                out=averages[what, group][:].rearrange("c k n -> c (k n)"),
+                lhsT=averager[:],
+                rhs=sums[what, group][:].rearrange("c k n -> c (k n)"),
+                start=True,
+                stop=True,
+            )
+
+        def take_moments(what, group, rows):
+            moments[what, group] = small.tile([P, 2, columns(group)], F32, name="moments")
+            nc.vector.tensor_scalar_mul(
+                out=moments[what, group][:], in0=averages[what, group][:], scalar1=WIDTH / rows
+            )
+
+        def square_mean(what, group):
+            mean_squared[what, group] = small.tile([P, columns(group)], F32, name="mean_squared")
+            mean = moments[what, group][:, 0, :]
+            nc.vector.tensor_mul(out=mean_squared[what, group][:], in0=mean, in1=mean)
+
+        def bound_squares(what, group):
+            variance[what, group] = small.tile([P, columns(group)], F32, name="variance")
+            nc.vector.tensor_max(
+                out=variance[what, group][:], in0=moments[what, group][:, 1, :], in1=mean_squared[what, group][:]
+            )
+
+        def subtract_mean(what, group):
+            nc.vector.tensor_sub(
+                out=variance[what, group][:], in0=variance[what, group][:], in1=mean_squared[what, group][:]
+            )
+
+        def take_root(what, group):
+            root[what, group] = small.tile([P, columns(group)], F32, name="root")
+            nc.gpsimd.tensor_tensor(
+                out=root[what, group][:], in0=variance[what, group][:], in1=half[:, 0 : columns(group)], op=ALU.pow
+            )
+
+        def add_eps(what, group, rows):
+            n = rows * WIDTH
+            nc.vector.tensor_scalar(
+                out=root[what, group][:], in0=root[what, group][:],
+                scalar1=math.sqrt(n / (n - 1.0)), scalar2=EPS, op0=ALU.mult, op1=ALU.add,
+            )
+
+        def invert(what, group):
+            inverse[what, group] = small.tile([P, columns(group)], F32, name="inverse")
+            nc.vector.reciprocal(out=inverse[what, group][:], in_=root[what, group][:])
+
+        tanh_z = {}
+        t_rows = {}
         t_turned = {}
         t_grouped = {}
 
-        def tanh_of_z(b):
-            if not exists(b):
-                return
-            tanh_z[b] = work.tile([P, HALVES, ROWS], F32, name="tanh_z")
-            sums[b] = small.tile([P, 2 * HALVES], F32, name="sums")
-            for h in range(HALVES):
-                nc.scalar.activation(
-                    out=tanh_z[b][:, h, :], in_=z[(b, h)][:], func=ACT.Tanh, accum_out=sums[b][:, h : h + 1]
-                )
+        def column(b, h):
+            c = HALVES * GROUPS[group_of(b)].index(b) + h
+            return slice(c, c + 1)
 
-        def squares_of_tanh(b):
-            if not exists(b):
-                return
-            for h in range(HALVES):
-                unread = work.tile([P, ROWS], BF16, name="unread_square")
-                nc.scalar.activation(
-                    out=unread[:],
-                    in_=tanh_z[b][:, h, :],
-                    func=ACT.Square,
-                    accum_out=sums[b][:, HALVES + h : HALVES + h + 1],
-                )
-
-        def average_over_matrices(b):
-            if not exists(b):
-                return
-            averages[b] = psum_avg.tile([P, 2 * HALVES], F32, name="averages", tag="avg")
-            nc.tensor.matmul(out=averages[b][:], lhsT=averager[:], rhs=sums[b][:], start=True, stop=True)
-
-        def t_statistics(b):
-            if not exists(b):
-                return
-            t_moments[b] = small.tile([P, 2 * HALVES], F32, name="t_moments")
-            nc.vector.tensor_copy(out=t_moments[b][:], in_=averages[b][:])
-            t_std[b] = std_plus_eps(
-                t_moments[b][:, 0:HALVES], t_moments[b][:, HALVES : 2 * HALVES], ROWS * WIDTH
+        def tanh_of_z(b, h):
+            if h == 0:
+                tanh_z[b] = tanh_pool.tile([P, HALVES, ROWS], F32, name="tanh_z")
+                if b == GROUPS[group_of(b)][0]:
+                    new_sums("t", group_of(b))
+            nc.scalar.activation(
+                out=tanh_z[b][:, h, :],
+                in_=z[(b, h)][:],
+                func=ACT.Tanh,
+                accum_out=sums["t", group_of(b)][:, 0, column(b, h)],
             )
 
-        t_inv = {}
-        t_rows = {}
+        def squares_of_tanh(b, h):
+            unread = work.tile([P, ROWS], BF16, name="unread_square")
+            nc.scalar.activation(
+                out=unread[:],
+                in_=tanh_z[b][:, h, :],
+                func=ACT.Square,
+                accum_out=sums["t", group_of(b)][:, 1, column(b, h)],
+            )
 
-        def invert_t_std(b):
-            if not exists(b):
-                return
-            t_inv[b] = small.tile([P, HALVES], F32, name="t_inv")
-            nc.vector.reciprocal(out=t_inv[b][:], in_=t_std[b][:])
+        def standardise_t(b, h):
+            if h == 0:
+                t_rows[b] = tanh_pool.tile([P, HALVES, ROWS], BF16, name="t_rows")
+            nc.vector.tensor_scalar(
+                out=t_rows[b][:, h, :],
+                in0=tanh_z[b][:, h, :],
+                scalar1=moments["t", group_of(b)][:, 0, column(b, h)],
+                scalar2=inverse["t", group_of(b)][:, column(b, h)],
+                op0=ALU.subtract,
+                op1=ALU.mult,
+            )
 
-        def standardise_t(b):
-            if not exists(b):
-                return
-            t_rows[b] = work.tile([P, HALVES, ROWS], BF16, name="t_rows")
-            for h in range(HALVES):
-                nc.vector.tensor_scalar(
-                    out=t_rows[b][:, h, :],
-                    in0=tanh_z[b][:, h, :],
-                    scalar1=t_moments[b][:, h : h + 1],
-                    scalar2=t_inv[b][:, h : h + 1],
-                    op0=ALU.subtract,
-                    op1=ALU.mult,
+        def transpose_t(b, h):
+            if h == 0:
+                t_turned[b] = psum_flip.tile([P, 2, ALL_WIDTH], F32, name="t_turned", tag="flip")
+            words = t_rows[b][:].rearrange("c h i -> c (h i)").bitcast(F32)
+            for u in range(2):
+                nc.tensor.transpose(
+                    t_turned[b][:, u, h * P : (h + 1) * P],
+                    words[:, h * ROWS // 2 + u : (h + 1) * ROWS // 2 : 2],
+                    identity[:],
                 )
 
-        def transpose_t(b):
-            if not exists(b):
-                return
-            t_turned[b] = psum_t.tile([P, 2, ALL_WIDTH], F32, name="t_turned", tag="t")
-            words = t_rows[b][:].rearrange("c h i -> c (h i)").bitcast(F32)
-            for h in range(HALVES):
-                for u in range(2):
-                    nc.tensor.transpose(
-                        t_turned[b][:, u, h * P : (h + 1) * P],
-                        words[:, h * ROWS // 2 + u : (h + 1) * ROWS // 2 : 2],
-                        identity[:],
-                    )
-
         def regroup_t(b, copy=nc.scalar.copy):
-            if not exists(b):
-                return
             t_grouped[b] = work.tile([P, ALL_WIDTH, PACK], BF16, name="t_grouped", align_bytes=64)
             copy(
                 out=t_grouped[b][:]
@@ -358,19 +362,10 @@ def tile_selfprojectiondev_pa_e_kernel(
         t_scales = {}
         u = {}
         tanh_u = {}
-        u_sums = {}
-        u_averages = {}
-        u_moments = {}
-        u_std = {}
-        u_inv = {}
+        squares_u = {}
         centred_u = {}
 
-        def closes_group(b):
-            return exists(b) and b % GROUP == GROUP - 1
-
         def quantise_t(b):
-            if not exists(b):
-                return
             t_codes[b] = work.tile([P, ALL_WIDTH], U32, name="t_codes", align_bytes=64)
             t_scales[b] = work.tile([P, ALL_WIDTH], U8, name="t_scales", align_bytes=64)
             nc.vector.quantize_mx(
@@ -380,11 +375,11 @@ def tile_selfprojectiondev_pa_e_kernel(
             )
 
         def second_product(b):
-            if not exists(b):
-                return
-            group, member = divmod(b, GROUP)
+            group = group_of(b)
+            member = GROUPS[group].index(b)
             if member == 0:
-                u[group] = psum_u.tile([P, GROUP, HALVES, P], F32, name="u", tag="u")
+                pool, tag = (psum_flip, "flip") if group == len(GROUPS) - 1 else (psum_u, "u")
+                u[group] = pool.tile([P, len(GROUPS[group]), HALVES, P], F32, name="u", tag=tag)
             for h in range(HALVES):
                 cols = slice(h * P, (h + 1) * P)
                 nc.tensor.matmul_mx(
@@ -397,210 +392,328 @@ def tile_selfprojectiondev_pa_e_kernel(
                     stop=True,
                 )
 
-        def tanh_of_u(b):
-            if not closes_group(b):
-                return
-            group = b // GROUP
-            tanh_u[group] = group_pool.tile([P, GROUP * HALVES, WIDTH], F32, name="tanh_u")
+        def tanh_of_u(group):
+            tanh_u[group] = group_pool.tile([P, columns(group), WIDTH], F32, name="tanh_u")
             by_pass = u[group][:].rearrange("c m h e -> c (m h) e")
             for k in range(DEPTHS_PER_HALF):
                 own = slice(k * WIDTH, (k + 1) * WIDTH)
                 nc.scalar.activation(out=tanh_u[group][own, :, :], in_=by_pass[own, :, own], func=ACT.Tanh)
 
-        squares_u = {}
-
-        def squares_of_u(b):
-            if not closes_group(b):
-                return
-            group = b // GROUP
-            squares_u[group] = group_pool.tile([P, GROUP * HALVES, WIDTH], F32, name="squares_u")
+        def squares_of_u(group):
+            squares_u[group] = group_pool.tile([P, columns(group), WIDTH], F32, name="squares_u")
             nc.scalar.activation(out=squares_u[group][:], in_=tanh_u[group][:], func=ACT.Square)
 
-        def sum_u(b):
-            if not closes_group(b):
-                return
-            group = b // GROUP
-            u_sums[group] = small.tile([P, 2, GROUP * HALVES], F32, name="u_sums")
-            nc.vector.reduce_sum(out=u_sums[group][:, 0, :], in_=tanh_u[group][:], axis=AXIS.X)
+        def sum_u(group):
+            new_sums("u", group)
+            nc.vector.reduce_sum(out=sums["u", group][:, 0, :], in_=tanh_u[group][:], axis=AXIS.X)
 
-        def sum_squares_of_u(b):
-            if not closes_group(b):
-                return
-            group = b // GROUP
-            nc.vector.reduce_sum(out=u_sums[group][:, 1, :], in_=squares_u[group][:], axis=AXIS.X)
+        def sum_squares_of_u(group):
+            nc.vector.reduce_sum(out=sums["u", group][:, 1, :], in_=squares_u[group][:], axis=AXIS.X)
 
-        def average_u(b):
-            if not closes_group(b):
-                return
-            group = b // GROUP
-            u_averages[group] = psum_avg.tile([P, 2, GROUP * HALVES], F32, name="u_averages", tag="avg")
-            nc.tensor.matmul(
-                out=u_averages[group][:].rearrange("c k n -> c (k n)"),
-                lhsT=averager[:],
-                rhs=u_sums[group][:].rearrange("c k n -> c (k n)"),
-                start=True,
-                stop=True,
-            )
+        def each_entry(group, values):
+            return values.unsqueeze(2).to_broadcast([P, columns(group), WIDTH])
 
-        def u_statistics(b):
-            if not closes_group(b):
-                return
-            group = b // GROUP
-            u_moments[group] = small.tile([P, 2, GROUP * HALVES], F32, name="u_moments")
-            nc.vector.tensor_scalar_mul(
-                out=u_moments[group][:], in0=u_averages[group][:], scalar1=float(ROWS // WIDTH)
-            )
-            u_std[group] = std_plus_eps(
-                u_moments[group][:, 0, :], u_moments[group][:, 1, :], WIDTH * WIDTH
-            )
-
-        def each_entry(columns):
-            return columns.unsqueeze(2).to_broadcast([P, GROUP * HALVES, WIDTH])
-
-        def centre_u(b):
-            if not closes_group(b):
-                return
-            group = b // GROUP
-            centred_u[group] = group_pool.tile([P, GROUP * HALVES, WIDTH], F32, name="centred_u")
+        def centre_u(group):
+            centred_u[group] = group_pool.tile([P, columns(group), WIDTH], F32, name="centred_u")
             nc.vector.tensor_sub(
-                out=centred_u[group][:], in0=tanh_u[group][:], in1=each_entry(u_moments[group][:, 0, :])
+                out=centred_u[group][:], in0=tanh_u[group][:], in1=each_entry(group, moments["u", group][:, 0, :])
             )
 
-        def invert_u_std(b):
-            if not closes_group(b):
-                return
-            group = b // GROUP
-            u_inv[group] = small.tile([P, GROUP * HALVES], F32, name="u_inv")
-            nc.vector.reciprocal(out=u_inv[group][:], in_=u_std[group][:])
-
-        def store_proj(b):
-            if not closes_group(b):
-                return
-            group = b // GROUP
-            proj = group_pool.tile([P, GROUP * HALVES, WIDTH], F32, name="proj")
-            nc.vector.tensor_mul(out=proj[:], in0=centred_u[group][:], in1=each_entry(u_inv[group][:]))
-            members = slice(group * GROUP, (group + 1) * GROUP)
+        def store_proj(group):
+            proj = group_pool.tile([P, columns(group), WIDTH], F32, name="proj")
+            nc.vector.tensor_mul(out=proj[:], in0=centred_u[group][:], in1=each_entry(group, inverse["u", group][:]))
+            members = slice(GROUPS[group][0], GROUPS[group][-1] + 1)
             nc.sync.dma_start(
                 out=out_0[members].rearrange("m (h k) w v -> (k w) (m h) v", h=HALVES), in_=proj[:]
             )
 
-        for piece in range(SET_PAIRS):
-            transpose_x(0, piece)
+        transpose_x(0, 0)
+        transpose_x(0, 1)
         regroup_x(0, 0)
-        regroup_x(0, 1, nc.scalar.copy)
         quantise_x(0, 0)
+        regroup_x(0, 1, nc.scalar.copy)
+        transpose_x(1, 0)
+        transpose_x(1, 1)
         quantise_x(0, 1)
-        for piece in range(SET_PAIRS):
-            transpose_x(1, piece)
-        project_o(0)
-        for piece in range(SET_PAIRS):
-            regroup_x(1, piece)
-            transpose_x(2, piece)
-        for piece in range(SET_PAIRS):
-            quantise_x(1, piece)
-        for s in range(BATCH):
-            regroup_x(s + 2, 0)
-            t_statistics(s - 1)
-            transpose_x(s + 3, 0)
-            regroup_x(s + 2, 1)
-            transpose_x(s + 3, 1)
-            invert_t_std(s - 2)
-            for piece in range(SET_PAIRS):
-                quantise_x(s + 2, piece)
-            quantise_t(s - 4)
-            tanh_of_z(s)
-            if s - 3 < 4:
-                regroup_t(s - 3)
-            project_o(s + 1)
-            second_product(s - 4)
-            project_rel(s - 6)
-            standardise_t(s - 2)
-            transpose_t(s - 2)
-            sum_u(s - 5)
-            sum_squares_of_u(s - 5)
-            average_u(s - 5)
-            row_max(s - 6, 0)
-            u_statistics(s - 5)
-            row_max(s - 6, 1)
-            centre_u(s - 5)
-            if s - 2 >= 4:
-                regroup_t(s - 2, nc.vector.tensor_copy)
-            squares_of_tanh(s)
-            average_over_matrices(s)
-            tanh_of_u(s - 4)
-            row_exp_sum(s - 6)
-            squares_of_u(s - 4)
-            invert_u_std(s - 6)
-            store_proj(s - 6)
-        invert_t_std(6)
-        project_rel(2)
-        quantise_t(4)
-        t_statistics(7)
-        standardise_t(6)
-        transpose_t(6)
-        second_product(4)
-        quantise_t(5)
-        second_product(5)
-        project_rel(3)
+        regroup_x(1, 0)
+        regroup_x(1, 1)
+        quantise_x(1, 0)
+        quantise_x(1, 1)
+        project_o(0, 0)
+        project_o(0, 1)
+        transpose_x(2, 0)
+        transpose_x(2, 1)
+        project_o(1, 0)
+        project_o(1, 1)
+        regroup_x(2, 0)
+        regroup_x(2, 1)
+        quantise_x(2, 0)
+        quantise_x(2, 1)
+        tanh_of_z(0, 0)
+        tanh_of_z(0, 1)
+        squares_of_tanh(0, 0)
+        squares_of_tanh(0, 1)
+        tanh_of_z(1, 0)
+        tanh_of_z(1, 1)
+        squares_of_tanh(1, 0)
+        squares_of_tanh(1, 1)
+        transpose_x(3, 0)
+        transpose_x(3, 1)
+        project_o(2, 0)
+        project_o(2, 1)
+        regroup_x(3, 0)
+        regroup_x(3, 1)
+        quantise_x(3, 0)
+        quantise_x(3, 1)
+        tanh_of_z(2, 0)
+        tanh_of_z(2, 1)
+        squares_of_tanh(2, 0)
+        squares_of_tanh(2, 1)
+        transpose_x(4, 0)
+        transpose_x(4, 1)
+        average("t", 0)
+        project_o(3, 0)
+        project_o(3, 1)
+        regroup_x(4, 0)
+        take_moments("t", 0, ROWS)
+        regroup_x(4, 1)
+        square_mean("t", 0)
+        quantise_x(4, 0)
+        quantise_x(4, 1)
+        bound_squares("t", 0)
+        tanh_of_z(3, 0)
+        tanh_of_z(3, 1)
+        squares_of_tanh(3, 0)
+        squares_of_tanh(3, 1)
+        transpose_x(5, 0)
+        transpose_x(5, 1)
+        project_o(4, 0)
+        project_o(4, 1)
+        regroup_x(5, 0)
+        subtract_mean("t", 0)
+        regroup_x(5, 1)
+        quantise_x(5, 0)
+        quantise_x(5, 1)
+        tanh_of_z(4, 0)
+        tanh_of_z(4, 1)
+        squares_of_tanh(4, 0)
+        squares_of_tanh(4, 1)
+        transpose_x(6, 0)
+        transpose_x(6, 1)
+        average("t", 1)
+        project_o(5, 0)
+        project_o(5, 1)
+        take_root("t", 0)
+        regroup_x(6, 0)
+        add_eps("t", 0, ROWS)
+        take_moments("t", 1, ROWS)
+        regroup_x(6, 1)
+        square_mean("t", 1)
+        invert("t", 0)
+        quantise_x(6, 0)
+        quantise_x(6, 1)
+        bound_squares("t", 1)
+        tanh_of_z(5, 0)
+        tanh_of_z(5, 1)
+        squares_of_tanh(5, 0)
+        squares_of_tanh(5, 1)
+        transpose_x(7, 0)
+        transpose_x(7, 1)
+        project_o(6, 0)
+        project_o(6, 1)
+        average("t", 2)
+        regroup_x(7, 0)
+        subtract_mean("t", 1)
+        regroup_x(7, 1)
+        quantise_x(7, 0)
+        quantise_x(7, 1)
+        standardise_t(0, 0)
+        standardise_t(0, 1)
+        tanh_of_z(6, 0)
+        tanh_of_z(6, 1)
+        squares_of_tanh(6, 0)
+        squares_of_tanh(6, 1)
+        project_o(7, 0)
+        project_o(7, 1)
+        transpose_t(0, 0)
+        transpose_t(0, 1)
+        take_root("t", 1)
+        add_eps("t", 1, ROWS)
+        standardise_t(1, 0)
+        standardise_t(1, 1)
+        invert("t", 1)
+        take_moments("t", 2, ROWS)
+        standardise_t(2, 0)
+        square_mean("t", 2)
+        standardise_t(2, 1)
+        bound_squares("t", 2)
+        standardise_t(3, 0)
+        subtract_mean("t", 2)
+        standardise_t(3, 1)
+        tanh_of_z(7, 0)
+        tanh_of_z(7, 1)
+        squares_of_tanh(7, 0)
+        squares_of_tanh(7, 1)
+        transpose_t(1, 0)
+        transpose_t(1, 1)
+        project_rel(0, 0)
+        project_rel(0, 1)
+        project_rel(1, 0)
+        project_rel(1, 1)
+        average("t", 3)
+        take_root("t", 2)
+        row_max(0, 0)
+        row_max(0, 1)
+        row_max(1, 0)
+        add_eps("t", 2, ROWS)
+        take_moments("t", 3, ROWS)
+        row_max(1, 1)
+        invert("t", 2)
+        square_mean("t", 3)
+        standardise_t(4, 0)
+        bound_squares("t", 3)
+        standardise_t(4, 1)
+        subtract_mean("t", 3)
+        standardise_t(5, 0)
+        standardise_t(5, 1)
+        row_exp_sum(0, 0)
+        row_exp_sum(0, 1)
+        row_exp_sum(1, 0)
+        row_exp_sum(1, 1)
+        regroup_t(0)
+        regroup_t(1)
+        project_rel(2, 0)
+        project_rel(2, 1)
+        transpose_t(2, 0)
+        transpose_t(2, 1)
+        project_rel(3, 0)
+        project_rel(3, 1)
+        transpose_t(3, 0)
+        transpose_t(3, 1)
+        take_root("t", 3)
         row_max(2, 0)
         row_max(2, 1)
-        regroup_t(6)
-        row_exp_sum(2)
-        store_mass(2)
+        quantise_t(0)
+        quantise_t(1)
         row_max(3, 0)
-        tanh_of_u(5)
-        squares_of_u(5)
-        project_rel(4)
+        add_eps("t", 3, ROWS)
+        row_max(3, 1)
+        invert("t", 3)
+        standardise_t(6, 0)
+        standardise_t(6, 1)
+        row_exp_sum(2, 0)
+        row_exp_sum(2, 1)
+        regroup_t(2)
+        regroup_t(3)
+        second_product(0)
+        second_product(1)
+        transpose_t(4, 0)
+        transpose_t(4, 1)
+        project_rel(4, 0)
+        project_rel(4, 1)
+        transpose_t(5, 0)
+        transpose_t(5, 1)
+        tanh_of_u(0)
+        squares_of_u(0)
+        row_exp_sum(3, 0)
+        row_exp_sum(3, 1)
+        regroup_t(4)
+        regroup_t(5)
+        sum_u(0)
+        sum_squares_of_u(0)
+        row_max(4, 0)
+        quantise_t(2)
+        quantise_t(3)
+        row_max(4, 1)
+        average("u", 0)
+        second_product(2)
+        second_product(3)
+        project_rel(5, 0)
+        project_rel(5, 1)
+        transpose_t(6, 0)
+        transpose_t(6, 1)
+        take_moments("u", 0, WIDTH)
+        standardise_t(7, 0)
+        square_mean("u", 0)
+        centre_u(0)
+        standardise_t(7, 1)
+        quantise_t(4)
+        bound_squares("u", 0)
+        quantise_t(5)
+        subtract_mean("u", 0)
+        row_max(5, 0)
+        tanh_of_u(1)
+        squares_of_u(1)
+        row_exp_sum(4, 0)
+        row_exp_sum(4, 1)
+        regroup_t(6)
+        transpose_t(7, 0)
+        transpose_t(7, 1)
+        second_product(4)
+        second_product(5)
+        take_root("u", 0)
+        sum_u(1)
+        sum_squares_of_u(1)
+        row_max(5, 1)
+        regroup_t(7)
+        tanh_of_u(2)
+        squares_of_u(2)
+        row_exp_sum(5, 0)
+        row_exp_sum(5, 1)
+        average("u", 1)
+        project_rel(6, 0)
+        project_rel(6, 1)
+        take_moments("u", 1, WIDTH)
+        quantise_t(6)
+        square_mean("u", 1)
+        centre_u(1)
+        quantise_t(7)
+        bound_squares("u", 1)
+        row_max(6, 0)
+        subtract_mean("u", 1)
+        add_eps("u", 0, WIDTH)
+        row_max(6, 1)
+        invert("u", 0)
+        sum_u(2)
+        sum_squares_of_u(2)
+        store_proj(0)
+        second_product(6)
+        second_product(7)
+        project_rel(7, 0)
+        project_rel(7, 1)
+        average("u", 2)
+        take_root("u", 1)
+        row_max(7, 0)
+        take_moments("u", 2, WIDTH)
+        add_eps("u", 1, WIDTH)
+        row_max(7, 1)
+        tanh_of_u(3)
+        squares_of_u(3)
+        row_exp_sum(6, 0)
+        row_exp_sum(6, 1)
+        row_exp_sum(7, 0)
+        row_exp_sum(7, 1)
         sum_u(3)
         sum_squares_of_u(3)
-        average_u(3)
-        invert_t_std(7)
-        quantise_t(6)
-        second_product(6)
-        standardise_t(7)
-        transpose_t(7)
-        u_statistics(3)
+        square_mean("u", 2)
+        centre_u(2)
+        invert("u", 1)
+        join_maxima()
+        bound_squares("u", 2)
+        store_proj(1)
+        average("u", 3)
+        take_moments("u", 3, WIDTH)
+        subtract_mean("u", 2)
+        square_mean("u", 3)
         centre_u(3)
-        row_max(3, 1)
-        sum_u(5)
-        sum_squares_of_u(5)
-        average_u(5)
-        row_exp_sum(3)
-        store_mass(3)
-        row_max(4, 0)
-        project_rel(5)
-        regroup_t(7)
-        u_statistics(5)
-        centre_u(5)
-        row_max(4, 1)
-        row_exp_sum(4)
-        store_mass(4)
-        quantise_t(7)
-        second_product(7)
-        project_rel(6)
-        row_max(5, 0)
-        row_max(5, 1)
-        tanh_of_u(7)
-        squares_of_u(7)
-        invert_u_std(3)
+        bound_squares("u", 3)
+        subtract_mean("u", 3)
+        store_mass()
+        take_root("u", 2)
+        take_root("u", 3)
+        add_eps("u", 2, WIDTH)
+        add_eps("u", 3, WIDTH)
+        invert("u", 2)
+        invert("u", 3)
+        store_proj(2)
         store_proj(3)
-        row_exp_sum(5)
-        store_mass(5)
-        row_max(6, 0)
-        project_rel(7)
-        sum_u(7)
-        sum_squares_of_u(7)
-        average_u(7)
-        row_max(6, 1)
-        u_statistics(7)
-        centre_u(7)
-        row_exp_sum(6)
-        store_mass(6)
-        row_max(7, 0)
-        row_max(7, 1)
-        invert_u_std(5)
-        store_proj(5)
-        row_exp_sum(7)
-        store_mass(7)
-        invert_u_std(7)
-        store_proj(7)

@@ -102,7 +102,7 @@ def tile_selfprojectiondev_pa_e_kernel(
 
         def load_x(b):
             x_rows[b] = x_pool.tile([P, PACK, COLS], BF16, name="x_rows")
-            by_set = x[b].rearrange("(a q) j -> q a j", a=PACK)
+            by_set = x[b].rearrange("(q a) j -> q a j", a=PACK)
             for piece in range(SET_PAIRS):
                 sets = slice(2 * piece, 2 * piece + 2)
                 nc.sync.dma_start(out=x_rows[b][:, sets, :], in_=by_set[:, sets, :])
@@ -110,15 +110,12 @@ def tile_selfprojectiondev_pa_e_kernel(
         load_x(0)
         load_codes(o_codes, o_xj_words)
         load_scales(o_plane, o_xj_scales)
-        load_x(1)
-        load_x(2)
+        for b in range(1, BATCH):
+            load_x(b)
         load_codes(rel_codes, rel_o_xj_words)
         load_scales(rel_plane, rel_o_xj_scales)
-        load_x(3)
         load_codes(p_codes, p_xj_words)
         load_scales(p_plane, p_xj_scales)
-        for b in range(4, BATCH):
-            load_x(b)
 
         flipped = {}
         x_grouped = {}
@@ -329,8 +326,8 @@ def tile_selfprojectiondev_pa_e_kernel(
             if h == 0:
                 t_rows[b] = tanh_pool.tile([P, HALVES, ROWS], BF16, name="t_rows")
             nc.vector.tensor_scalar(
-                out=t_rows[b][:, h, :],
-                in0=tanh_z[b][:, h, :],
+                out=t_rows[b][:, h, :].rearrange("c (u q e) -> c u q e", u=2, e=2),
+                in0=tanh_z[b][:, h, :].rearrange("c (u e q) -> c u q e", u=2, e=2),
                 scalar1=moments["t", group_of(b)][:, 0, column(b, h)],
                 scalar2=inverse["t", group_of(b)][:, column(b, h)],
                 op0=ALU.subtract,
@@ -344,7 +341,7 @@ def tile_selfprojectiondev_pa_e_kernel(
             for u in range(2):
                 nc.tensor.transpose(
                     t_turned[b][:, u, h * P : (h + 1) * P],
-                    words[:, h * ROWS // 2 + u : (h + 1) * ROWS // 2 : 2],
+                    words[:, (2 * h + u) * P : (2 * h + u + 1) * P],
                     identity[:],
                 )
 

@@ -29,7 +29,10 @@ ALL_WIDTH = DEPTHS * WIDTH
 HALVES = ALL_WIDTH // P
 DEPTHS_PER_HALF = DEPTHS // HALVES
 WORDS = COLS // 2
-GROUPS = ((0, 1), (2, 3), (4, 5), (6, 7))
+PAIR = 2
+GROUP = P // WIDTH
+PAIR_WIDTH = 2 * WIDTH
+COLUMNS = {"t": PAIR * HALVES, "u": DEPTHS}
 SET_PAIRS = PACK // 2
 PIECE = ROWS // SET_PAIRS
 
@@ -57,8 +60,8 @@ def tile_selfprojectiondev_pa_e_kernel(
         x_pool = stack.enter_context(tc.tile_pool(name="x_pool", bufs=BATCH))
         work = stack.enter_context(tc.tile_pool(name="work", bufs=4))
         tanh_pool = stack.enter_context(tc.tile_pool(name="tanh_pool", bufs=BATCH))
-        small = stack.enter_context(tc.tile_pool(name="small", bufs=2 * len(GROUPS)))
-        group_pool = stack.enter_context(tc.tile_pool(name="group_pool", bufs=len(GROUPS)))
+        small = stack.enter_context(tc.tile_pool(name="small", bufs=BATCH))
+        group_pool = stack.enter_context(tc.tile_pool(name="group_pool", bufs=BATCH // GROUP))
         psum_flip = stack.enter_context(tc.psum_pool(name="psum_flip", bufs=2))
         psum_first = stack.enter_context(tc.psum_pool(name="psum_first", bufs=4))
         psum_avg = stack.enter_context(tc.psum_pool(name="psum_avg", bufs=1))
@@ -71,7 +74,7 @@ def tile_selfprojectiondev_pa_e_kernel(
         for k in range(DEPTHS_PER_HALF):
             block = slice(k * WIDTH, (k + 1) * WIDTH)
             nc.vector.memset(averager[block, block], 1.0 / (WIDTH * WIDTH))
-        half = const.tile([P, 2 * HALVES], F32)
+        half = const.tile([P, PAIR * HALVES], F32)
         nc.vector.memset(half[:], 0.5)
 
         planes = const.tile([P, 3, ALL_WIDTH], U8, align_bytes=64)
@@ -203,23 +206,35 @@ def tile_selfprojectiondev_pa_e_kernel(
         neg_top = const.tile([P, 1], F32)
         rescale = const.tile([P, WIDTH], F32)
 
-        def join_maxima():
+        def turn_maxima():
             nc.vector.transpose(out=neg_max_t[:], in_=neg_max[:])
+
+        def join_maxima():
             nc.vector.tensor_reduce(out=neg_top[:], in_=neg_max_t[:], axis=AXIS.X, op=ALU.min)
+
+        def rescale_by_maxima():
             nc.scalar.activation(
                 out=rescale[:], in_=neg_max_t[:], func=ACT.Exp, bias=neg_top[:], scale=-1.0
             )
 
-        def store_mass():
-            exp_sum_t = const.tile([P, QUADRANT], F32, align_bytes=64)
+        exp_sum_t = const.tile([P, QUADRANT], F32, align_bytes=64)
+        mass = const.tile([P, WIDTH], F32)
+        denominator = const.tile([P, 1], F32)
+
+        def turn_sums():
             nc.vector.transpose(out=exp_sum_t[:], in_=exp_sum[:])
-            unnormalised = const.tile([P, WIDTH], F32)
-            nc.vector.tensor_mul(out=unnormalised[:], in0=rescale[:], in1=exp_sum_t[:])
-            denominator = const.tile([P, 1], F32)
-            nc.vector.reduce_sum(out=denominator[:], in_=unnormalised[:], axis=AXIS.X)
+
+        def rescale_sums():
+            nc.vector.tensor_mul(out=mass[:], in0=rescale[:], in1=exp_sum_t[:])
+
+        def total_mass():
+            nc.vector.reduce_sum(out=denominator[:], in_=mass[:], axis=AXIS.X)
+
+        def invert_total():
             nc.vector.reciprocal(out=denominator[:], in_=denominator[:])
-            mass = const.tile([P, WIDTH], F32)
-            nc.vector.tensor_scalar_mul(out=mass[:], in0=unnormalised[:], scalar1=denominator[:])
+
+        def store_mass():
+            nc.vector.tensor_scalar_mul(out=mass[:], in0=mass[:], scalar1=denominator[:])
             by_depth = out_1.rearrange("b (h k) w -> k (b h) w", k=DEPTHS_PER_HALF)
             for k in range(DEPTHS_PER_HALF):
                 nc.sync.dma_start(
@@ -234,17 +249,11 @@ def tile_selfprojectiondev_pa_e_kernel(
         root = {}
         inverse = {}
 
-        def group_of(b):
-            return [b in group for group in GROUPS].index(True)
-
-        def columns(group):
-            return len(GROUPS[group]) * HALVES
-
         def new_sums(what, group):
-            sums[what, group] = small.tile([P, 2, columns(group)], F32, name="sums")
+            sums[what, group] = small.tile([P, 2, COLUMNS[what]], F32, name="sums")
 
         def average(what, group):
-            averages[what, group] = psum_avg.tile([P, 2, columns(group)], F32, name="averages", tag="avg")
+            averages[what, group] = psum_avg.tile([P, 2, COLUMNS[what]], F32, name="averages", tag="avg")
             nc.tensor.matmul(
                 out=averages[what, group][:].rearrange("c k n -> c (k n)"),
                 lhsT=averager[:],
@@ -254,18 +263,18 @@ def tile_selfprojectiondev_pa_e_kernel(
             )
 
         def take_moments(what, group, rows):
-            moments[what, group] = small.tile([P, 2, columns(group)], F32, name="moments")
+            moments[what, group] = small.tile([P, 2, COLUMNS[what]], F32, name="moments")
             nc.vector.tensor_scalar_mul(
                 out=moments[what, group][:], in0=averages[what, group][:], scalar1=WIDTH / rows
             )
 
         def square_mean(what, group):
-            mean_squared[what, group] = small.tile([P, columns(group)], F32, name="mean_squared")
+            mean_squared[what, group] = small.tile([P, COLUMNS[what]], F32, name="mean_squared")
             mean = moments[what, group][:, 0, :]
             nc.vector.tensor_mul(out=mean_squared[what, group][:], in0=mean, in1=mean)
 
         def bound_squares(what, group):
-            variance[what, group] = small.tile([P, columns(group)], F32, name="variance")
+            variance[what, group] = small.tile([P, COLUMNS[what]], F32, name="variance")
             nc.vector.tensor_max(
                 out=variance[what, group][:], in0=moments[what, group][:, 1, :], in1=mean_squared[what, group][:]
             )
@@ -276,10 +285,17 @@ def tile_selfprojectiondev_pa_e_kernel(
             )
 
         def take_root(what, group):
-            root[what, group] = small.tile([P, columns(group)], F32, name="root")
-            nc.gpsimd.tensor_tensor(
-                out=root[what, group][:], in0=variance[what, group][:], in1=half[:, 0 : columns(group)], op=ALU.pow
-            )
+            root[what, group] = small.tile([P, COLUMNS[what]], F32, name="root")
+            if what == "t":
+                nc.gpsimd.tensor_tensor(
+                    out=root[what, group][:], in0=variance[what, group][:], in1=half[:], op=ALU.pow
+                )
+            else:
+                nc.scalar.activation(out=root[what, group][:], in_=variance[what, group][:], func=ACT.Sqrt)
+
+        def load_sqrt():
+            unread = small.tile([P, 1], F32, name="unread_root")
+            nc.scalar.activation(out=unread[:], in_=half[:, 0:1], func=ACT.Sqrt)
 
         def add_eps(what, group, rows):
             n = rows * WIDTH
@@ -289,7 +305,7 @@ def tile_selfprojectiondev_pa_e_kernel(
             )
 
         def invert(what, group):
-            inverse[what, group] = small.tile([P, columns(group)], F32, name="inverse")
+            inverse[what, group] = small.tile([P, COLUMNS[what]], F32, name="inverse")
             nc.vector.reciprocal(out=inverse[what, group][:], in_=root[what, group][:])
 
         tanh_z = {}
@@ -298,19 +314,19 @@ def tile_selfprojectiondev_pa_e_kernel(
         t_grouped = {}
 
         def column(b, h):
-            c = HALVES * GROUPS[group_of(b)].index(b) + h
+            c = HALVES * (b % PAIR) + h
             return slice(c, c + 1)
 
         def tanh_of_z(b, h):
             if h == 0:
                 tanh_z[b] = tanh_pool.tile([P, HALVES, ROWS], F32, name="tanh_z")
-                if b == GROUPS[group_of(b)][0]:
-                    new_sums("t", group_of(b))
+                if b % PAIR == 0:
+                    new_sums("t", b // PAIR)
             nc.scalar.activation(
                 out=tanh_z[b][:, h, :],
                 in_=z[(b, h)][:],
                 func=ACT.Tanh,
-                accum_out=sums["t", group_of(b)][:, 0, column(b, h)],
+                accum_out=sums["t", b // PAIR][:, 0, column(b, h)],
             )
 
         def squares_of_tanh(b, h):
@@ -319,7 +335,7 @@ def tile_selfprojectiondev_pa_e_kernel(
                 out=unread[:],
                 in_=tanh_z[b][:, h, :],
                 func=ACT.Square,
-                accum_out=sums["t", group_of(b)][:, 1, column(b, h)],
+                accum_out=sums["t", b // PAIR][:, 1, column(b, h)],
             )
 
         def standardise_t(b, h):
@@ -328,8 +344,8 @@ def tile_selfprojectiondev_pa_e_kernel(
             nc.vector.tensor_scalar(
                 out=t_rows[b][:, h, :].rearrange("c (u q e) -> c u q e", u=2, e=2),
                 in0=tanh_z[b][:, h, :].rearrange("c (u e q) -> c u q e", u=2, e=2),
-                scalar1=moments["t", group_of(b)][:, 0, column(b, h)],
-                scalar2=inverse["t", group_of(b)][:, column(b, h)],
+                scalar1=moments["t", b // PAIR][:, 0, column(b, h)],
+                scalar2=inverse["t", b // PAIR][:, column(b, h)],
                 op0=ALU.subtract,
                 op1=ALU.mult,
             )
@@ -346,14 +362,18 @@ def tile_selfprojectiondev_pa_e_kernel(
                 )
 
         def regroup_t(b, copy=nc.scalar.copy):
-            t_grouped[b] = work.tile([P, ALL_WIDTH, PACK], BF16, name="t_grouped", align_bytes=64)
-            copy(
-                out=t_grouped[b][:]
-                .rearrange("q c a -> q (c a)")
+            group, member = divmod(b, GROUP)
+            if member == 0:
+                t_grouped[group] = group_pool.tile(
+                    [P, DEPTHS, GROUP, WIDTH * PACK], BF16, name="t_grouped", align_bytes=64
+                )
+            out = (
+                t_grouped[group][:]
+                .rearrange("q d m e -> q (d m e)")
                 .bitcast(F32)
-                .rearrange("q (c u) -> q c u", u=2),
-                in_=t_turned[b][:].rearrange("q u c -> q c u"),
+                .rearrange("q (d m w u) -> q d m w u", d=DEPTHS, m=GROUP, u=2)[:, :, member, :, :]
             )
+            copy(out=out, in_=t_turned[b][:].rearrange("q u (d w) -> q d w u", d=DEPTHS))
 
         t_codes = {}
         t_scales = {}
@@ -362,42 +382,43 @@ def tile_selfprojectiondev_pa_e_kernel(
         squares_u = {}
         centred_u = {}
 
-        def quantise_t(b):
-            t_codes[b] = work.tile([P, ALL_WIDTH], U32, name="t_codes", align_bytes=64)
-            t_scales[b] = work.tile([P, ALL_WIDTH], U8, name="t_scales", align_bytes=64)
+        def quantise_t(group, h):
+            if h == 0:
+                t_codes[group] = group_pool.tile([P, DEPTHS * P], U32, name="t_codes", align_bytes=64)
+                t_scales[group] = group_pool.tile([P, DEPTHS * P], U8, name="t_scales", align_bytes=64)
+            depths = slice(h * DEPTHS_PER_HALF, (h + 1) * DEPTHS_PER_HALF)
+            cols = slice(h * DEPTHS_PER_HALF * P, (h + 1) * DEPTHS_PER_HALF * P)
             nc.vector.quantize_mx(
-                out=t_codes[b][:].bitcast(FP8X4),
-                scales=t_scales[b][:],
-                in_=t_grouped[b][:].rearrange("q c a -> q (c a)"),
+                out=t_codes[group][:, cols].bitcast(FP8X4),
+                scales=t_scales[group][:, cols],
+                in_=t_grouped[group][:, depths, :, :].rearrange("q d m e -> q (d m e)"),
             )
 
-        def second_product(b):
-            group = group_of(b)
-            member = GROUPS[group].index(b)
-            if member == 0:
-                pool, tag = (psum_flip, "flip") if group == len(GROUPS) - 1 else (psum_u, "u")
-                u[group] = pool.tile([P, len(GROUPS[group]), HALVES, P], F32, name="u", tag=tag)
-            for h in range(HALVES):
-                cols = slice(h * P, (h + 1) * P)
+        def second_product(group, h):
+            if h == 0:
+                u[group] = psum_u.tile([P, DEPTHS, PAIR_WIDTH], F32, name="u")
+            for d in range(h * DEPTHS_PER_HALF, (h + 1) * DEPTHS_PER_HALF):
+                members = slice(d * P, (d + 1) * P)
+                pair = slice((d // 2) * PAIR_WIDTH, (d // 2 + 1) * PAIR_WIDTH)
                 nc.tensor.matmul_mx(
-                    out=u[group][:, member, h, :],
-                    lhsT=t_codes[b][:, cols].bitcast(FP8X4),
-                    lhsT_scale=t_scales[b][:, cols],
-                    rhs=p_codes[:, cols].bitcast(FP8X4),
-                    rhs_scale=p_plane[:, cols],
+                    out=u[group][:, d, :],
+                    lhsT=t_codes[group][:, members].bitcast(FP8X4),
+                    lhsT_scale=t_scales[group][:, members],
+                    rhs=p_codes[:, pair].bitcast(FP8X4),
+                    rhs_scale=p_plane[:, pair],
                     start=True,
                     stop=True,
                 )
 
         def tanh_of_u(group):
-            tanh_u[group] = group_pool.tile([P, columns(group), WIDTH], F32, name="tanh_u")
-            by_pass = u[group][:].rearrange("c m h e -> c (m h) e")
-            for k in range(DEPTHS_PER_HALF):
-                own = slice(k * WIDTH, (k + 1) * WIDTH)
-                nc.scalar.activation(out=tanh_u[group][own, :, :], in_=by_pass[own, :, own], func=ACT.Tanh)
+            own = u[group][:].rearrange("q (e f) (g v) -> q e (f g) v", f=2, g=2)[:, :, 0:4:3, :]
+            tanh_u[group] = group_pool.tile([P, DEPTHS, WIDTH], F32, name="tanh_u")
+            nc.scalar.activation(
+                out=tanh_u[group][:].rearrange("q (e f) v -> q e f v", f=2), in_=own, func=ACT.Tanh
+            )
 
         def squares_of_u(group):
-            squares_u[group] = group_pool.tile([P, columns(group), WIDTH], F32, name="squares_u")
+            squares_u[group] = group_pool.tile([P, DEPTHS, WIDTH], F32, name="squares_u")
             nc.scalar.activation(out=squares_u[group][:], in_=tanh_u[group][:], func=ACT.Square)
 
         def sum_u(group):
@@ -407,22 +428,23 @@ def tile_selfprojectiondev_pa_e_kernel(
         def sum_squares_of_u(group):
             nc.vector.reduce_sum(out=sums["u", group][:, 1, :], in_=squares_u[group][:], axis=AXIS.X)
 
-        def each_entry(group, values):
-            return values.unsqueeze(2).to_broadcast([P, columns(group), WIDTH])
+        def each_entry(values):
+            return values.unsqueeze(2).to_broadcast([P, DEPTHS, WIDTH])
 
         def centre_u(group):
-            centred_u[group] = group_pool.tile([P, columns(group), WIDTH], F32, name="centred_u")
+            centred_u[group] = group_pool.tile([P, DEPTHS, WIDTH], F32, name="centred_u")
             nc.vector.tensor_sub(
-                out=centred_u[group][:], in0=tanh_u[group][:], in1=each_entry(group, moments["u", group][:, 0, :])
+                out=centred_u[group][:], in0=tanh_u[group][:], in1=each_entry(moments["u", group][:, 0, :])
             )
 
         def store_proj(group):
-            proj = group_pool.tile([P, columns(group), WIDTH], F32, name="proj")
-            nc.vector.tensor_mul(out=proj[:], in0=centred_u[group][:], in1=each_entry(group, inverse["u", group][:]))
-            members = slice(GROUPS[group][0], GROUPS[group][-1] + 1)
-            nc.sync.dma_start(
-                out=out_0[members].rearrange("m (h k) w v -> (k w) (m h) v", h=HALVES), in_=proj[:]
-            )
+            proj = group_pool.tile([P, DEPTHS, WIDTH], F32, name="proj")
+            nc.vector.tensor_mul(out=proj[:], in0=centred_u[group][:], in1=each_entry(inverse["u", group][:]))
+            for member in range(GROUP):
+                nc.sync.dma_start(
+                    out=out_0[group * GROUP + member].rearrange("d w v -> w d v"),
+                    in_=proj[member * WIDTH : (member + 1) * WIDTH, :, :],
+                )
 
         transpose_x(0, 0)
         transpose_x(0, 1)
@@ -590,127 +612,98 @@ def tile_selfprojectiondev_pa_e_kernel(
         take_root("t", 3)
         row_max(2, 0)
         row_max(2, 1)
-        quantise_t(0)
-        quantise_t(1)
         row_max(3, 0)
         add_eps("t", 3, ROWS)
         row_max(3, 1)
         invert("t", 3)
         standardise_t(6, 0)
         standardise_t(6, 1)
+        standardise_t(7, 0)
+        standardise_t(7, 1)
         row_exp_sum(2, 0)
         row_exp_sum(2, 1)
         regroup_t(2)
         regroup_t(3)
-        second_product(0)
-        second_product(1)
+        row_exp_sum(3, 0)
+        row_exp_sum(3, 1)
         transpose_t(4, 0)
         transpose_t(4, 1)
         project_rel(4, 0)
         project_rel(4, 1)
         transpose_t(5, 0)
         transpose_t(5, 1)
-        tanh_of_u(0)
-        squares_of_u(0)
-        row_exp_sum(3, 0)
-        row_exp_sum(3, 1)
-        regroup_t(4)
-        regroup_t(5)
-        sum_u(0)
-        sum_squares_of_u(0)
-        row_max(4, 0)
-        quantise_t(2)
-        quantise_t(3)
-        row_max(4, 1)
-        average("u", 0)
-        second_product(2)
-        second_product(3)
         project_rel(5, 0)
         project_rel(5, 1)
+        quantise_t(0, 0)
+        row_max(4, 0)
+        quantise_t(0, 1)
+        row_max(4, 1)
+        row_max(5, 0)
+        row_max(5, 1)
+        regroup_t(4)
+        regroup_t(5)
+        row_exp_sum(4, 0)
         transpose_t(6, 0)
         transpose_t(6, 1)
-        take_moments("u", 0, WIDTH)
-        standardise_t(7, 0)
-        square_mean("u", 0)
-        centre_u(0)
-        standardise_t(7, 1)
-        quantise_t(4)
-        bound_squares("u", 0)
-        quantise_t(5)
-        subtract_mean("u", 0)
-        row_max(5, 0)
-        tanh_of_u(1)
-        squares_of_u(1)
-        row_exp_sum(4, 0)
-        row_exp_sum(4, 1)
-        regroup_t(6)
         transpose_t(7, 0)
         transpose_t(7, 1)
-        second_product(4)
-        second_product(5)
-        take_root("u", 0)
-        sum_u(1)
-        sum_squares_of_u(1)
-        row_max(5, 1)
-        regroup_t(7)
-        tanh_of_u(2)
-        squares_of_u(2)
+        second_product(0, 0)
+        second_product(0, 1)
+        project_rel(6, 0)
+        regroup_t(7, nc.vector.tensor_copy)
+        regroup_t(6)
+        row_exp_sum(4, 1)
+        tanh_of_u(0)
+        squares_of_u(0)
         row_exp_sum(5, 0)
         row_exp_sum(5, 1)
-        average("u", 1)
-        project_rel(6, 0)
         project_rel(6, 1)
-        take_moments("u", 1, WIDTH)
-        quantise_t(6)
-        square_mean("u", 1)
-        centre_u(1)
-        quantise_t(7)
-        bound_squares("u", 1)
+        quantise_t(1, 0)
+        quantise_t(1, 1)
+        sum_u(0)
         row_max(6, 0)
-        subtract_mean("u", 1)
-        add_eps("u", 0, WIDTH)
+        sum_squares_of_u(0)
         row_max(6, 1)
-        invert("u", 0)
-        sum_u(2)
-        sum_squares_of_u(2)
-        store_proj(0)
-        second_product(6)
-        second_product(7)
+        second_product(1, 0)
+        second_product(1, 1)
         project_rel(7, 0)
         project_rel(7, 1)
-        average("u", 2)
-        take_root("u", 1)
+        average("u", 0)
         row_max(7, 0)
-        take_moments("u", 2, WIDTH)
-        add_eps("u", 1, WIDTH)
         row_max(7, 1)
-        tanh_of_u(3)
-        squares_of_u(3)
+        tanh_of_u(1)
+        squares_of_u(1)
         row_exp_sum(6, 0)
         row_exp_sum(6, 1)
         row_exp_sum(7, 0)
         row_exp_sum(7, 1)
-        sum_u(3)
-        sum_squares_of_u(3)
-        square_mean("u", 2)
-        centre_u(2)
-        invert("u", 1)
+        sum_u(1)
+        turn_maxima()
+        sum_squares_of_u(1)
+        take_moments("u", 0, WIDTH)
         join_maxima()
-        bound_squares("u", 2)
-        store_proj(1)
-        average("u", 3)
-        take_moments("u", 3, WIDTH)
-        subtract_mean("u", 2)
-        square_mean("u", 3)
-        centre_u(3)
-        bound_squares("u", 3)
-        subtract_mean("u", 3)
+        square_mean("u", 0)
+        centre_u(0)
+        bound_squares("u", 0)
+        rescale_by_maxima()
+        load_sqrt()
+        average("u", 1)
+        take_moments("u", 1, WIDTH)
+        subtract_mean("u", 0)
+        square_mean("u", 1)
+        centre_u(1)
+        turn_sums()
+        bound_squares("u", 1)
+        rescale_sums()
+        subtract_mean("u", 1)
+        total_mass()
+        take_root("u", 0)
+        take_root("u", 1)
+        add_eps("u", 0, WIDTH)
+        invert_total()
+        add_eps("u", 1, WIDTH)
         store_mass()
-        take_root("u", 2)
-        take_root("u", 3)
-        add_eps("u", 2, WIDTH)
-        add_eps("u", 3, WIDTH)
-        invert("u", 2)
-        invert("u", 3)
-        store_proj(2)
-        store_proj(3)
+        invert("u", 0)
+        invert("u", 1)
+        store_proj(0)
+        store_proj(1)

@@ -62,10 +62,9 @@ def tile_selfprojectiondev_pa_e_kernel(
         tanh_pool = stack.enter_context(tc.tile_pool(name="tanh_pool", bufs=BATCH))
         small = stack.enter_context(tc.tile_pool(name="small", bufs=BATCH))
         group_pool = stack.enter_context(tc.tile_pool(name="group_pool", bufs=BATCH // GROUP))
-        psum_flip = stack.enter_context(tc.psum_pool(name="psum_flip", bufs=2))
+        psum_flip = stack.enter_context(tc.psum_pool(name="psum_flip", bufs=3))
         psum_first = stack.enter_context(tc.psum_pool(name="psum_first", bufs=4))
         psum_avg = stack.enter_context(tc.psum_pool(name="psum_avg", bufs=1))
-        psum_u = stack.enter_context(tc.psum_pool(name="psum_u", bufs=1))
 
         identity = const.tile([P, P], F32)
         make_identity(nc, identity[:])
@@ -180,10 +179,10 @@ def tile_selfprojectiondev_pa_e_kernel(
         def project_rel(b, h):
             project(r, b, h, "r", psum_first, "first", rel_codes, rel_plane)
 
-        neg_max = const.tile([P, QUADRANT], F32, align_bytes=64)
-        nc.vector.memset(neg_max[:], 0.0)
-        exp_sum = const.tile([P, QUADRANT], F32, align_bytes=64)
-        nc.vector.memset(exp_sum[:], 1.0)
+        neg_max = const.tile([P, P], F32)
+        nc.gpsimd.memset(neg_max[:], 0.0)
+        exp_sum = const.tile([P, P], F32)
+        nc.gpsimd.memset(exp_sum[:], 1.0)
 
         def row_max(b, h):
             c = HALVES * b + h
@@ -202,44 +201,48 @@ def tile_selfprojectiondev_pa_e_kernel(
                 accum_out=exp_sum[:, c : c + 1],
             )
 
-        neg_max_t = const.tile([P, QUADRANT], F32, align_bytes=64)
-        neg_top = const.tile([P, 1], F32)
-        rescale = const.tile([P, WIDTH], F32)
+        turned = {}
+        neg_top = const.tile([P, DEPTHS_PER_HALF], F32)
+        rescale = const.tile([P, DEPTHS_PER_HALF, WIDTH], F32)
+        mass = const.tile([P, DEPTHS_PER_HALF, WIDTH], F32)
+        total = const.tile([P, DEPTHS_PER_HALF], F32)
+
+        def each_width(values):
+            return values.unsqueeze(2).to_broadcast([P, DEPTHS_PER_HALF, WIDTH])
+
+        def turn(what, columns):
+            turned[what] = psum_flip.tile([P, DEPTHS_PER_HALF, WIDTH], F32, name="turned", tag="flip")
+            nc.tensor.transpose(turned[what][:].rearrange("c k w -> c (k w)"), columns[:], identity[:])
 
         def turn_maxima():
-            nc.vector.transpose(out=neg_max_t[:], in_=neg_max[:])
+            turn("maxima", neg_max)
 
         def join_maxima():
-            nc.vector.tensor_reduce(out=neg_top[:], in_=neg_max_t[:], axis=AXIS.X, op=ALU.min)
+            nc.vector.tensor_reduce(out=neg_top[:], in_=turned["maxima"][:], axis=AXIS.X, op=ALU.min)
+
+        def shift_by_maxima():
+            nc.vector.tensor_sub(out=rescale[:], in0=each_width(neg_top[:]), in1=turned["maxima"][:])
 
         def rescale_by_maxima():
-            nc.scalar.activation(
-                out=rescale[:], in_=neg_max_t[:], func=ACT.Exp, bias=neg_top[:], scale=-1.0
-            )
-
-        exp_sum_t = const.tile([P, QUADRANT], F32, align_bytes=64)
-        mass = const.tile([P, WIDTH], F32)
-        denominator = const.tile([P, 1], F32)
+            nc.scalar.activation(out=rescale[:], in_=rescale[:], func=ACT.Exp)
 
         def turn_sums():
-            nc.vector.transpose(out=exp_sum_t[:], in_=exp_sum[:])
+            turn("sums", exp_sum)
 
         def rescale_sums():
-            nc.vector.tensor_mul(out=mass[:], in0=rescale[:], in1=exp_sum_t[:])
+            nc.vector.tensor_mul(out=mass[:], in0=rescale[:], in1=turned["sums"][:])
 
         def total_mass():
-            nc.vector.reduce_sum(out=denominator[:], in_=mass[:], axis=AXIS.X)
+            nc.vector.reduce_sum(out=total[:], in_=mass[:], axis=AXIS.X)
 
         def invert_total():
-            nc.vector.reciprocal(out=denominator[:], in_=denominator[:])
+            nc.vector.reciprocal(out=total[:], in_=total[:])
 
         def store_mass():
-            nc.vector.tensor_scalar_mul(out=mass[:], in0=mass[:], scalar1=denominator[:])
-            by_depth = out_1.rearrange("b (h k) w -> k (b h) w", k=DEPTHS_PER_HALF)
-            for k in range(DEPTHS_PER_HALF):
-                nc.sync.dma_start(
-                    out=by_depth[k], in_=mass[QUADRANT * k : QUADRANT * k + HALVES * BATCH, :]
-                )
+            nc.vector.tensor_mul(out=mass[:], in0=mass[:], in1=each_width(total[:]))
+            nc.sync.dma_start(
+                out=out_1.rearrange("b (h k) w -> (b h) k w", h=HALVES), in_=mass[0 : HALVES * BATCH, :, :]
+            )
 
         sums = {}
         averages = {}
@@ -396,7 +399,7 @@ def tile_selfprojectiondev_pa_e_kernel(
 
         def second_product(group, h):
             if h == 0:
-                u[group] = psum_u.tile([P, DEPTHS, PAIR_WIDTH], F32, name="u")
+                u[group] = psum_flip.tile([P, DEPTHS, PAIR_WIDTH], F32, name="u", tag="flip")
             for d in range(h * DEPTHS_PER_HALF, (h + 1) * DEPTHS_PER_HALF):
                 members = slice(d * P, (d + 1) * P)
                 pair = slice((d // 2) * PAIR_WIDTH, (d // 2 + 1) * PAIR_WIDTH)
@@ -448,10 +451,10 @@ def tile_selfprojectiondev_pa_e_kernel(
 
         transpose_x(0, 0)
         transpose_x(0, 1)
+        transpose_x(1, 0)
         regroup_x(0, 0)
         quantise_x(0, 0)
         regroup_x(0, 1, nc.scalar.copy)
-        transpose_x(1, 0)
         transpose_x(1, 1)
         quantise_x(0, 1)
         regroup_x(1, 0)
@@ -464,10 +467,12 @@ def tile_selfprojectiondev_pa_e_kernel(
         transpose_x(2, 1)
         project_o(1, 0)
         project_o(1, 1)
+        transpose_x(3, 0)
         regroup_x(2, 0)
         regroup_x(2, 1)
         quantise_x(2, 0)
         quantise_x(2, 1)
+        regroup_x(3, 0)
         tanh_of_z(0, 0)
         tanh_of_z(0, 1)
         squares_of_tanh(0, 0)
@@ -476,23 +481,15 @@ def tile_selfprojectiondev_pa_e_kernel(
         tanh_of_z(1, 1)
         squares_of_tanh(1, 0)
         squares_of_tanh(1, 1)
-        transpose_x(3, 0)
         transpose_x(3, 1)
         project_o(2, 0)
         project_o(2, 1)
-        regroup_x(3, 0)
-        regroup_x(3, 1)
-        quantise_x(3, 0)
-        quantise_x(3, 1)
-        tanh_of_z(2, 0)
-        tanh_of_z(2, 1)
-        squares_of_tanh(2, 0)
-        squares_of_tanh(2, 1)
         transpose_x(4, 0)
         transpose_x(4, 1)
         average("t", 0)
-        project_o(3, 0)
-        project_o(3, 1)
+        regroup_x(3, 1)
+        quantise_x(3, 0)
+        quantise_x(3, 1)
         regroup_x(4, 0)
         take_moments("t", 0, ROWS)
         regroup_x(4, 1)
@@ -500,30 +497,38 @@ def tile_selfprojectiondev_pa_e_kernel(
         quantise_x(4, 0)
         quantise_x(4, 1)
         bound_squares("t", 0)
-        tanh_of_z(3, 0)
-        tanh_of_z(3, 1)
-        squares_of_tanh(3, 0)
-        squares_of_tanh(3, 1)
+        tanh_of_z(2, 0)
+        tanh_of_z(2, 1)
+        squares_of_tanh(2, 0)
+        squares_of_tanh(2, 1)
+        project_o(3, 0)
+        project_o(3, 1)
         transpose_x(5, 0)
         transpose_x(5, 1)
         project_o(4, 0)
         project_o(4, 1)
+        transpose_x(6, 0)
         regroup_x(5, 0)
         subtract_mean("t", 0)
         regroup_x(5, 1)
         quantise_x(5, 0)
         quantise_x(5, 1)
+        regroup_x(6, 0)
+        tanh_of_z(3, 0)
+        tanh_of_z(3, 1)
+        squares_of_tanh(3, 0)
+        squares_of_tanh(3, 1)
         tanh_of_z(4, 0)
         tanh_of_z(4, 1)
         squares_of_tanh(4, 0)
         squares_of_tanh(4, 1)
-        transpose_x(6, 0)
         transpose_x(6, 1)
         average("t", 1)
         project_o(5, 0)
         project_o(5, 1)
+        transpose_x(7, 0)
+        transpose_x(7, 1)
         take_root("t", 0)
-        regroup_x(6, 0)
         add_eps("t", 0, ROWS)
         take_moments("t", 1, ROWS)
         regroup_x(6, 1)
@@ -532,15 +537,6 @@ def tile_selfprojectiondev_pa_e_kernel(
         quantise_x(6, 0)
         quantise_x(6, 1)
         bound_squares("t", 1)
-        tanh_of_z(5, 0)
-        tanh_of_z(5, 1)
-        squares_of_tanh(5, 0)
-        squares_of_tanh(5, 1)
-        transpose_x(7, 0)
-        transpose_x(7, 1)
-        project_o(6, 0)
-        project_o(6, 1)
-        average("t", 2)
         regroup_x(7, 0)
         subtract_mean("t", 1)
         regroup_x(7, 1)
@@ -548,10 +544,13 @@ def tile_selfprojectiondev_pa_e_kernel(
         quantise_x(7, 1)
         standardise_t(0, 0)
         standardise_t(0, 1)
-        tanh_of_z(6, 0)
-        tanh_of_z(6, 1)
-        squares_of_tanh(6, 0)
-        squares_of_tanh(6, 1)
+        tanh_of_z(5, 0)
+        tanh_of_z(5, 1)
+        squares_of_tanh(5, 0)
+        squares_of_tanh(5, 1)
+        project_o(6, 0)
+        project_o(6, 1)
+        average("t", 2)
         project_o(7, 0)
         project_o(7, 1)
         transpose_t(0, 0)
@@ -569,6 +568,10 @@ def tile_selfprojectiondev_pa_e_kernel(
         standardise_t(3, 0)
         subtract_mean("t", 2)
         standardise_t(3, 1)
+        tanh_of_z(6, 0)
+        tanh_of_z(6, 1)
+        squares_of_tanh(6, 0)
+        squares_of_tanh(6, 1)
         tanh_of_z(7, 0)
         tanh_of_z(7, 1)
         squares_of_tanh(7, 0)
@@ -609,6 +612,8 @@ def tile_selfprojectiondev_pa_e_kernel(
         project_rel(3, 1)
         transpose_t(3, 0)
         transpose_t(3, 1)
+        transpose_t(4, 0)
+        transpose_t(4, 1)
         take_root("t", 3)
         row_max(2, 0)
         row_max(2, 1)
@@ -626,49 +631,46 @@ def tile_selfprojectiondev_pa_e_kernel(
         regroup_t(3)
         row_exp_sum(3, 0)
         row_exp_sum(3, 1)
-        transpose_t(4, 0)
-        transpose_t(4, 1)
+        regroup_t(4)
         project_rel(4, 0)
         project_rel(4, 1)
         transpose_t(5, 0)
         transpose_t(5, 1)
         project_rel(5, 0)
         project_rel(5, 1)
+        transpose_t(6, 0)
+        transpose_t(6, 1)
+        transpose_t(7, 0)
+        transpose_t(7, 1)
         quantise_t(0, 0)
         row_max(4, 0)
         quantise_t(0, 1)
         row_max(4, 1)
         row_max(5, 0)
         row_max(5, 1)
-        regroup_t(4)
+        regroup_t(7, nc.vector.tensor_copy)
         regroup_t(5)
         row_exp_sum(4, 0)
-        transpose_t(6, 0)
-        transpose_t(6, 1)
-        transpose_t(7, 0)
-        transpose_t(7, 1)
+        regroup_t(6)
+        row_exp_sum(4, 1)
         second_product(0, 0)
         second_product(0, 1)
         project_rel(6, 0)
-        regroup_t(7, nc.vector.tensor_copy)
-        regroup_t(6)
-        row_exp_sum(4, 1)
+        project_rel(6, 1)
+        quantise_t(1, 0)
+        quantise_t(1, 1)
         tanh_of_u(0)
         squares_of_u(0)
         row_exp_sum(5, 0)
         row_exp_sum(5, 1)
-        project_rel(6, 1)
-        quantise_t(1, 0)
-        quantise_t(1, 1)
-        sum_u(0)
-        row_max(6, 0)
-        sum_squares_of_u(0)
-        row_max(6, 1)
         second_product(1, 0)
         second_product(1, 1)
         project_rel(7, 0)
         project_rel(7, 1)
-        average("u", 0)
+        sum_u(0)
+        row_max(6, 0)
+        sum_squares_of_u(0)
+        row_max(6, 1)
         row_max(7, 0)
         row_max(7, 1)
         tanh_of_u(1)
@@ -677,33 +679,35 @@ def tile_selfprojectiondev_pa_e_kernel(
         row_exp_sum(6, 1)
         row_exp_sum(7, 0)
         row_exp_sum(7, 1)
-        sum_u(1)
+        average("u", 0)
         turn_maxima()
+        sum_u(1)
         sum_squares_of_u(1)
         take_moments("u", 0, WIDTH)
         join_maxima()
+        shift_by_maxima()
         square_mean("u", 0)
-        centre_u(0)
         bound_squares("u", 0)
         rescale_by_maxima()
         load_sqrt()
         average("u", 1)
+        turn_sums()
         take_moments("u", 1, WIDTH)
         subtract_mean("u", 0)
         square_mean("u", 1)
-        centre_u(1)
-        turn_sums()
-        bound_squares("u", 1)
         rescale_sums()
-        subtract_mean("u", 1)
+        bound_squares("u", 1)
         total_mass()
+        subtract_mean("u", 1)
+        centre_u(0)
+        invert_total()
+        centre_u(1)
         take_root("u", 0)
         take_root("u", 1)
         add_eps("u", 0, WIDTH)
-        invert_total()
         add_eps("u", 1, WIDTH)
-        store_mass()
         invert("u", 0)
         invert("u", 1)
+        store_mass()
         store_proj(0)
         store_proj(1)

@@ -332,6 +332,18 @@ def tile_selfprojectiondev_pa_e_kernel(
                 accum_out=sums["t", b // PAIR][:, 0, column(b, h)],
             )
 
+        def squares_of_tanh_on_vector(b, h):
+            unread = work.tile([P, ROWS], BF16, name="unread_product")
+            nc.vector.scalar_tensor_tensor(
+                out=unread[:],
+                in0=tanh_z[b][:, h, :],
+                scalar=1.0,
+                in1=tanh_z[b][:, h, :],
+                op0=ALU.mult,
+                op1=ALU.mult,
+                accum_out=sums["t", b // PAIR][:, 1, column(b, h)],
+            )
+
         def squares_of_tanh(b, h):
             unread = work.tile([P, ROWS], BF16, name="unread_square")
             nc.scalar.activation(
@@ -500,7 +512,6 @@ def tile_selfprojectiondev_pa_e_kernel(
         tanh_of_z(2, 0)
         tanh_of_z(2, 1)
         squares_of_tanh(2, 0)
-        squares_of_tanh(2, 1)
         project_o(3, 0)
         project_o(3, 1)
         transpose_x(5, 0)
@@ -511,6 +522,7 @@ def tile_selfprojectiondev_pa_e_kernel(
         regroup_x(5, 0)
         subtract_mean("t", 0)
         regroup_x(5, 1)
+        squares_of_tanh_on_vector(2, 1)
         quantise_x(5, 0)
         quantise_x(5, 1)
         regroup_x(6, 0)
@@ -588,15 +600,15 @@ def tile_selfprojectiondev_pa_e_kernel(
         row_max(0, 1)
         row_max(1, 0)
         add_eps("t", 2, ROWS)
-        take_moments("t", 3, ROWS)
         row_max(1, 1)
         invert("t", 2)
-        square_mean("t", 3)
+        take_moments("t", 3, ROWS)
         standardise_t(4, 0)
-        bound_squares("t", 3)
+        square_mean("t", 3)
         standardise_t(4, 1)
-        subtract_mean("t", 3)
+        bound_squares("t", 3)
         standardise_t(5, 0)
+        subtract_mean("t", 3)
         standardise_t(5, 1)
         row_exp_sum(0, 0)
         row_exp_sum(0, 1)
@@ -648,10 +660,10 @@ def tile_selfprojectiondev_pa_e_kernel(
         row_max(4, 1)
         row_max(5, 0)
         row_max(5, 1)
-        regroup_t(7, nc.vector.tensor_copy)
         regroup_t(5)
         row_exp_sum(4, 0)
         regroup_t(6)
+        regroup_t(7)
         row_exp_sum(4, 1)
         second_product(0, 0)
         second_product(0, 1)

import math
from contextlib import ExitStack

import concourse.mybir as mybir
from concourse.masks import make_identity

F32 = mybir.dt.float32
BF16 = mybir.dt.bfloat16
I32 = mybir.dt.int32
U32 = mybir.dt.uint32
U8 = mybir.dt.uint8
FP8X4 = mybir.dt.float8_e4m3fn_x4
ACT = mybir.ActivationFunctionType
ALU = mybir.AluOpType
AXIS = mybir.AxisListType

P = 128
PACK = 4
QUADRANT = 32

BATCH = 8
ROWS = 512
COLS = 512
DEPTHS = 8
WIDTH = 32
EPS = 1e-5

ALL_WIDTH = DEPTHS * WIDTH
HALVES = ALL_WIDTH // P
DEPTHS_PER_HALF = DEPTHS // HALVES
WORDS = COLS // 2
PAIR = 2
GROUP = P // WIDTH
PAIR_WIDTH = 2 * WIDTH
COLUMNS = {"t": PAIR * HALVES, "u": DEPTHS}
SET_PAIRS = PACK // 2
PIECE = ROWS // SET_PAIRS

LAG = 4

FLOPS = 2 * BATCH * DEPTHS * (2 * ROWS * COLS * WIDTH + ROWS * WIDTH * WIDTH)


def tile_selfprojectiondev_pa_e_kernel(
    tc,
    x,
    o_xj_words,
    o_xj_scales,
    p_xj_words,
    p_xj_scales,
    rel_o_xj_words,
    rel_o_xj_scales,
    out_0,
    out_1,
):
    nc = tc.nc
    with ExitStack() as stack:
        stack.enter_context(tc.manual_schedule())
        const = stack.enter_context(tc.tile_pool(name="const", bufs=1))
        x_pool = stack.enter_context(tc.tile_pool(name="x_pool", bufs=BATCH))
        work = stack.enter_context(tc.tile_pool(name="work", bufs=4))
        tanh_pool = stack.enter_context(tc.tile_pool(name="tanh_pool", bufs=BATCH))
        small = stack.enter_context(tc.tile_pool(name="small", bufs=BATCH))
        group_pool = stack.enter_context(tc.tile_pool(name="group_pool", bufs=BATCH // GROUP))
        psum_flip = stack.enter_context(tc.psum_pool(name="psum_flip", bufs=3))
        psum_first = stack.enter_context(tc.psum_pool(name="psum_first", bufs=4))
        psum_avg = stack.enter_context(tc.psum_pool(name="psum_avg", bufs=1))

        identity = const.tile([P, P], F32)
        make_identity(nc, identity[:])
        averager = const.tile([P, P], F32)
        nc.vector.memset(averager[:], 0.0)
        for k in range(DEPTHS_PER_HALF):
            block = slice(k * WIDTH, (k + 1) * WIDTH)
            nc.vector.memset(averager[block, block], 1.0 / (WIDTH * WIDTH))
        half = const.tile([P, PAIR * HALVES], F32)
        nc.vector.memset(half[:], 0.5)

        planes = const.tile([P, 3, ALL_WIDTH], U8, align_bytes=64)
        nc.vector.memset(planes[:].rearrange("q k n -> q (k n)").bitcast(I32), 0)
        o_plane, rel_plane, p_plane = planes[:, 0, :], planes[:, 1, :], planes[:, 2, :]
        o_codes = const.tile([P, ALL_WIDTH], U32, align_bytes=64)
        rel_codes = const.tile([P, ALL_WIDTH], U32, align_bytes=64)
        p_codes = const.tile([P, ALL_WIDTH], U32, align_bytes=64)

        def load_codes(codes, words):
            nc.sync.dma_start(
                out=codes[:].bitcast(I32).rearrange("q (d n) -> q d n", d=DEPTHS),
                in_=words.rearrange("d q n t -> q d (n t)").bitcast(I32),
            )

        def load_scales(plane, scales):
            for quad in range(P // QUADRANT):
                nc.sync.dma_start(
                    out=plane[QUADRANT * quad : QUADRANT * quad + PACK, :]
                    .bitcast(I32)
                    .rearrange("r (d n) -> r d n", d=DEPTHS),
                    in_=scales[:, PACK * quad : PACK * (quad + 1), :]
                    .rearrange("d r n -> r d n")
                    .bitcast(I32),
                )

        x_rows = {}

        def load_x(b):
            x_rows[b] = x_pool.tile([P, PACK, COLS], BF16, name="x_rows")
            by_set = x[b].rearrange("(q a) j -> q a j", a=PACK)
            for piece in range(SET_PAIRS):
                sets = slice(2 * piece, 2 * piece + 2)
                nc.sync.dma_start(out=x_rows[b][:, sets, :], in_=by_set[:, sets, :])

        load_x(0)
        load_codes(o_codes, o_xj_words)
        load_scales(o_plane, o_xj_scales)
        for b in range(1, BATCH):
            load_x(b)
        load_codes(rel_codes, rel_o_xj_words)
        load_scales(rel_plane, rel_o_xj_scales)
        load_codes(p_codes, p_xj_words)
        load_scales(p_plane, p_xj_scales)

        flipped = {}
        x_grouped = {}
        x_codes = {}
        x_scales = {}

        def transpose_x(b, piece):
            words = x_rows[b][:].rearrange("q a j -> q (a j)").bitcast(F32)
            flipped[(b, piece)] = psum_flip.tile([P, 2, PIECE], F32, name="flipped", tag="flip")
            for a2 in range(2):
                a = 2 * piece + a2
                for u in range(2):
                    nc.tensor.transpose(
                        flipped[(b, piece)][:, u, a2 * P : (a2 + 1) * P],
                        words[:, a * WORDS + u : (a + 1) * WORDS : 2],
                        identity[:],
                    )

        def regroup_x(b, piece, copy=nc.vector.tensor_copy):
            x_grouped[(b, piece)] = work.tile([P, PIECE, PACK], BF16, name="x_grouped", align_bytes=64)
            copy(
                out=x_grouped[(b, piece)][:]
                .rearrange("k c t -> k (c t)")
                .bitcast(F32)
                .rearrange("k (c u) -> k c u", u=2),
                in_=flipped[(b, piece)][:].rearrange("k u c -> k c u"),
            )

        def quantise_x(b, piece):
            if piece == 0:
                x_codes[b] = x_pool.tile([P, ROWS], U32, name="x_codes", align_bytes=64)
                x_scales[b] = x_pool.tile([P, ROWS], U8, name="x_scales", align_bytes=64)
            rows = slice(piece * PIECE, (piece + 1) * PIECE)
            nc.vector.quantize_mx(
                out=x_codes[b][:, rows].bitcast(FP8X4),
                scales=x_scales[b][:, rows],
                in_=x_grouped[(b, piece)][:].rearrange("k c t -> k (c t)"),
            )

        z = {}
        r = {}

        def project(product, b, h, name, pool, tag, codes, plane):
            cols = slice(h * P, (h + 1) * P)
            product[(b, h)] = pool.tile([P, ROWS], F32, name=name, tag=tag)
            nc.tensor.matmul_mx(
                out=product[(b, h)][:],
                lhsT=codes[:, cols].bitcast(FP8X4),
                lhsT_scale=plane[:, cols],
                rhs=x_codes[b][:].bitcast(FP8X4),
                rhs_scale=x_scales[b][:],
                start=True,
                stop=True,
            )

        def project_o(b, h):
            project(z, b, h, "z", psum_first, "first", o_codes, o_plane)

        def project_rel(b, h):
            project(r, b, h, "r", psum_first, "first", rel_codes, rel_plane)

        neg_max = const.tile([P, P], F32)
        nc.gpsimd.memset(neg_max[:], 0.0)
        exp_sum = const.tile([P, P], F32)
        nc.gpsimd.memset(exp_sum[:], 1.0)

        def row_max(b, h):
            c = HALVES * b + h
            nc.vector.tensor_reduce(
                out=neg_max[:, c : c + 1], in_=r[(b, h)][:], axis=AXIS.X, op=ALU.max, negate=True
            )

        def row_exp_sum(b, h):
            c = HALVES * b + h
            unread = work.tile([P, ROWS], BF16, name="unread_exp")
            nc.scalar.activation(
                out=unread[:],
                in_=r[(b, h)][:],
                func=ACT.Exp,
                bias=neg_max[:, c : c + 1],
                accum_out=exp_sum[:, c : c + 1],
            )

        turned = {}
        neg_top = const.tile([P, DEPTHS_PER_HALF], F32)
        rescale = const.tile([P, DEPTHS_PER_HALF, WIDTH], F32)
        mass = const.tile([P, DEPTHS_PER_HALF, WIDTH], F32)
        total = const.tile([P, DEPTHS_PER_HALF], F32)

        def each_width(values):
            return values.unsqueeze(2).to_broadcast([P, DEPTHS_PER_HALF, WIDTH])

        def turn(what, columns):
            turned[what] = psum_flip.tile([P, DEPTHS_PER_HALF, WIDTH], F32, name="turned", tag="flip")
            nc.tensor.transpose(turned[what][:].rearrange("c k w -> c (k w)"), columns[:], identity[:])

        def turn_maxima():
            turn("maxima", neg_max)

        def join_maxima():
            nc.vector.tensor_reduce(out=neg_top[:], in_=turned["maxima"][:], axis=AXIS.X, op=ALU.min)

        def shift_by_maxima():
            nc.vector.tensor_sub(out=rescale[:], in0=each_width(neg_top[:]), in1=turned["maxima"][:])

        def rescale_by_maxima():
            nc.scalar.activation(out=rescale[:], in_=rescale[:], func=ACT.Exp)

        def turn_sums():
            turn("sums", exp_sum)

        def rescale_sums():
            nc.vector.tensor_mul(out=mass[:], in0=rescale[:], in1=turned["sums"][:])

        def total_mass():
            nc.vector.reduce_sum(out=total[:], in_=mass[:], axis=AXIS.X)

        def invert_total():
            nc.vector.reciprocal(out=total[:], in_=total[:])

        def store_mass():
            nc.vector.tensor_mul(out=mass[:], in0=mass[:], in1=each_width(total[:]))
            nc.sync.dma_start(
                out=out_1.rearrange("b (h k) w -> (b h) k w", h=HALVES), in_=mass[0 : HALVES * BATCH, :, :]
            )

        sums = {}
        averages = {}
        moments = {}
        mean_squared = {}
        variance = {}
        root = {}
        inverse = {}

        def new_sums(what, group):
            sums[what, group] = small.tile([P, 2, COLUMNS[what]], F32, name="sums")

        def average(what, group):
            averages[what, group] = psum_avg.tile([P, 2, COLUMNS[what]], F32, name="averages", tag="avg")
            nc.tensor.matmul(
                out=averages[what, group][:].rearrange("c k n -> c (k n)"),
                lhsT=averager[:],
                rhs=sums[what, group][:].rearrange("c k n -> c (k n)"),
                start=True,
                stop=True,
            )

        def take_moments(what, group, rows):
            moments[what, group] = small.tile([P, 2, COLUMNS[what]], F32, name="moments")
            nc.vector.tensor_scalar_mul(
                out=moments[what, group][:], in0=averages[what, group][:], scalar1=WIDTH / rows
            )

        def square_mean(what, group):
            mean_squared[what, group] = small.tile([P, COLUMNS[what]], F32, name="mean_squared")
            mean = moments[what, group][:, 0, :]
            nc.vector.tensor_mul(out=mean_squared[what, group][:], in0=mean, in1=mean)

        def bound_squares(what, group):
            variance[what, group] = small.tile([P, COLUMNS[what]], F32, name="variance")
            nc.vector.tensor_max(
                out=variance[what, group][:], in0=moments[what, group][:, 1, :], in1=mean_squared[what, group][:]
            )

        def subtract_mean(what, group):
            nc.vector.tensor_sub(
                out=variance[what, group][:], in0=variance[what, group][:], in1=mean_squared[what, group][:]
            )

        def take_root(what, group):
            root[what, group] = small.tile([P, COLUMNS[what]], F32, name="root")
            if what == "t":
                nc.gpsimd.tensor_tensor(
                    out=root[what, group][:], in0=variance[what, group][:], in1=half[:], op=ALU.pow
                )
            else:
                nc.scalar.activation(out=root[what, group][:], in_=variance[what, group][:], func=ACT.Sqrt)

        def load_sqrt():
            unread = small.tile([P, 1], F32, name="unread_root")
            nc.scalar.activation(out=unread[:], in_=half[:, 0:1], func=ACT.Sqrt)

        def add_eps(what, group, rows):
            n = rows * WIDTH
            nc.vector.tensor_scalar(
                out=root[what, group][:], in0=root[what, group][:],
                scalar1=math.sqrt(n / (n - 1.0)), scalar2=EPS, op0=ALU.mult, op1=ALU.add,
            )

        def invert(what, group):
            inverse[what, group] = small.tile([P, COLUMNS[what]], F32, name="inverse")
            nc.vector.reciprocal(out=inverse[what, group][:], in_=root[what, group][:])

        tanh_z = {}
        t_rows = {}
        t_turned = {}
        t_grouped = {}

        def column(b, h):
            c = HALVES * (b % PAIR) + h
            return slice(c, c + 1)

        def tanh_of_z(b, h):
            if h == 0:
                tanh_z[b] = tanh_pool.tile([P, HALVES, ROWS], F32, name="tanh_z")
                if b % PAIR == 0:
                    new_sums("t", b // PAIR)
            nc.scalar.activation(
                out=tanh_z[b][:, h, :],
                in_=z[(b, h)][:],
                func=ACT.Tanh,
                accum_out=sums["t", b // PAIR][:, 0, column(b, h)],
            )

        def squares_of_tanh_on_vector(b, h):
            unread = work.tile([P, ROWS], BF16, name="unread_product")
            nc.vector.scalar_tensor_tensor(
                out=unread[:],
                in0=tanh_z[b][:, h, :],
                scalar=1.0,
                in1=tanh_z[b][:, h, :],
                op0=ALU.mult,
                op1=ALU.mult,
                accum_out=sums["t", b // PAIR][:, 1, column(b, h)],
            )

        def squares_of_tanh(b, h):
            unread = work.tile([P, ROWS], BF16, name="unread_square")
            nc.scalar.activation(
                out=unread[:],
                in_=tanh_z[b][:, h, :],
                func=ACT.Square,
                accum_out=sums["t", b // PAIR][:, 1, column(b, h)],
            )

        def standardise_t(b, h):
            if h == 0:
                t_rows[b] = tanh_pool.tile([P, HALVES, ROWS], BF16, name="t_rows")
            nc.vector.tensor_scalar(
                out=t_rows[b][:, h, :].rearrange("c (u q e) -> c u q e", u=2, e=2),
                in0=tanh_z[b][:, h, :].rearrange("c (u e q) -> c u q e", u=2, e=2),
                scalar1=moments["t", b // PAIR][:, 0, column(b, h)],
                scalar2=inverse["t", b // PAIR][:, column(b, h)],
                op0=ALU.subtract,
                op1=ALU.mult,
            )

        def transpose_t(b, h):
            if h == 0:
                t_turned[b] = psum_flip.tile([P, 2, ALL_WIDTH], F32, name="t_turned", tag="flip")
            words = t_rows[b][:].rearrange("c h i -> c (h i)").bitcast(F32)
            for u in range(2):
                nc.tensor.transpose(
                    t_turned[b][:, u, h * P : (h + 1) * P],
                    words[:, (2 * h + u) * P : (2 * h + u + 1) * P],
                    identity[:],
                )

        def regroup_t(b, copy=nc.scalar.copy):
            group, member = divmod(b, GROUP)
            if member == 0:
                t_grouped[group] = group_pool.tile(
                    [P, DEPTHS, GROUP, WIDTH * PACK], BF16, name="t_grouped", align_bytes=64
                )
            out = (
                t_grouped[group][:]
                .rearrange("q d m e -> q (d m e)")
                .bitcast(F32)
                .rearrange("q (d m w u) -> q d m w u", d=DEPTHS, m=GROUP, u=2)[:, :, member, :, :]
            )
            copy(out=out, in_=t_turned[b][:].rearrange("q u (d w) -> q d w u", d=DEPTHS))

        t_codes = {}
        t_scales = {}
        u = {}
        tanh_u = {}
        squares_u = {}
        centred_u = {}

        def quantise_t(group, h):
            if h == 0:
                t_codes[group] = group_pool.tile([P, DEPTHS * P], U32, name="t_codes", align_bytes=64)
                t_scales[group] = group_pool.tile([P, DEPTHS * P], U8, name="t_scales", align_bytes=64)
            depths = slice(h * DEPTHS_PER_HALF, (h + 1) * DEPTHS_PER_HALF)
            cols = slice(h * DEPTHS_PER_HALF * P, (h + 1) * DEPTHS_PER_HALF * P)
            nc.vector.quantize_mx(
                out=t_codes[group][:, cols].bitcast(FP8X4),
                scales=t_scales[group][:, cols],
                in_=t_grouped[group][:, depths, :, :].rearrange("q d m e -> q (d m e)"),
            )

        def second_product(group, h):
            if h == 0:
                u[group] = psum_flip.tile([P, DEPTHS, PAIR_WIDTH], F32, name="u", tag="flip")
            for d in range(h * DEPTHS_PER_HALF, (h + 1) * DEPTHS_PER_HALF):
                members = slice(d * P, (d + 1) * P)
                pair = slice((d // 2) * PAIR_WIDTH, (d // 2 + 1) * PAIR_WIDTH)
                nc.tensor.matmul_mx(
                    out=u[group][:, d, :],
                    lhsT=t_codes[group][:, members].bitcast(FP8X4),
                    lhsT_scale=t_scales[group][:, members],
                    rhs=p_codes[:, pair].bitcast(FP8X4),
                    rhs_scale=p_plane[:, pair],
                    start=True,
                    stop=True,
                )

        def tanh_of_u(group):
            own = u[group][:].rearrange("q (e f) (g v) -> q e (f g) v", f=2, g=2)[:, :, 0:4:3, :]
            tanh_u[group] = group_pool.tile([P, DEPTHS, WIDTH], F32, name="tanh_u")
            nc.scalar.activation(
                out=tanh_u[group][:].rearrange("q (e f) v -> q e f v", f=2), in_=own, func=ACT.Tanh
            )

        def squares_of_u(group):
            squares_u[group] = group_pool.tile([P, DEPTHS, WIDTH], F32, name="squares_u")
            nc.scalar.activation(out=squares_u[group][:], in_=tanh_u[group][:], func=ACT.Square)

        def sum_u(group):
            new_sums("u", group)
            nc.vector.reduce_sum(out=sums["u", group][:, 0, :], in_=tanh_u[group][:], axis=AXIS.X)

        def sum_squares_of_u(group):
            nc.vector.reduce_sum(out=sums["u", group][:, 1, :], in_=squares_u[group][:], axis=AXIS.X)

        def each_entry(values):
            return values.unsqueeze(2).to_broadcast([P, DEPTHS, WIDTH])

        def centre_u(group):
            centred_u[group] = group_pool.tile([P, DEPTHS, WIDTH], F32, name="centred_u")
            nc.vector.tensor_sub(
                out=centred_u[group][:], in0=tanh_u[group][:], in1=each_entry(moments["u", group][:, 0, :])
            )

        def store_proj(group):
            proj = group_pool.tile([P, DEPTHS, WIDTH], F32, name="proj")
            nc.vector.tensor_mul(out=proj[:], in0=centred_u[group][:], in1=each_entry(inverse["u", group][:]))
            for member in range(GROUP):
                nc.sync.dma_start(
                    out=out_0[group * GROUP + member].rearrange("d w v -> w d v"),
                    in_=proj[member * WIDTH : (member + 1) * WIDTH, :, :],
                )

        transpose_x(0, 0)
        transpose_x(0, 1)
        transpose_x(1, 0)
        regroup_x(0, 0)
        quantise_x(0, 0)
        regroup_x(0, 1, nc.scalar.copy)
        transpose_x(1, 1)
        quantise_x(0, 1)
        regroup_x(1, 0)
        regroup_x(1, 1)
        quantise_x(1, 0)
        quantise_x(1, 1)
        project_o(0, 0)
        project_o(0, 1)
        transpose_x(2, 0)
        transpose_x(2, 1)
        project_o(1, 0)
        project_o(1, 1)
        transpose_x(3, 0)
        regroup_x(2, 0)
        regroup_x(2, 1)
        quantise_x(2, 0)
        quantise_x(2, 1)
        regroup_x(3, 0)
        tanh_of_z(0, 0)
        tanh_of_z(0, 1)
        squares_of_tanh(0, 0)
        squares_of_tanh(0, 1)
        tanh_of_z(1, 0)
        tanh_of_z(1, 1)
        squares_of_tanh(1, 0)
        squares_of_tanh(1, 1)
        transpose_x(3, 1)
        project_o(2, 0)
        project_o(2, 1)
        transpose_x(4, 0)
        transpose_x(4, 1)
        average("t", 0)
        regroup_x(3, 1)
        quantise_x(3, 0)
        quantise_x(3, 1)
        regroup_x(4, 0)
        take_moments("t", 0, ROWS)
        regroup_x(4, 1)
        square_mean("t", 0)
        quantise_x(4, 0)
        quantise_x(4, 1)
        bound_squares("t", 0)
        tanh_of_z(2, 0)
        tanh_of_z(2, 1)
        squares_of_tanh(2, 0)
        project_o(3, 0)
        project_o(3, 1)
        transpose_x(5, 0)
        transpose_x(5, 1)
        project_o(4, 0)
        project_o(4, 1)
        transpose_x(6, 0)
        regroup_x(5, 0)
        subtract_mean("t", 0)
        regroup_x(5, 1)
        squares_of_tanh_on_vector(2, 1)
        quantise_x(5, 0)
        quantise_x(5, 1)
        regroup_x(6, 0)
        tanh_of_z(3, 0)
        tanh_of_z(3, 1)
        squares_of_tanh(3, 0)
        squares_of_tanh(3, 1)
        tanh_of_z(4, 0)
        tanh_of_z(4, 1)
        squares_of_tanh(4, 0)
        squares_of_tanh(4, 1)
        transpose_x(6, 1)
        average("t", 1)
        project_o(5, 0)
        project_o(5, 1)
        transpose_x(7, 0)
        transpose_x(7, 1)
        take_root("t", 0)
        add_eps("t", 0, ROWS)
        take_moments("t", 1, ROWS)
        regroup_x(6, 1)
        square_mean("t", 1)
        invert("t", 0)
        quantise_x(6, 0)
        quantise_x(6, 1)
        bound_squares("t", 1)
        regroup_x(7, 0)
        subtract_mean("t", 1)
        regroup_x(7, 1)
        quantise_x(7, 0)
        quantise_x(7, 1)
        standardise_t(0, 0)
        standardise_t(0, 1)
        tanh_of_z(5, 0)
        tanh_of_z(5, 1)
        squares_of_tanh(5, 0)
        squares_of_tanh(5, 1)
        project_o(6, 0)
        project_o(6, 1)
        average("t", 2)
        project_o(7, 0)
        project_o(7, 1)
        transpose_t(0, 0)
        transpose_t(0, 1)
        take_root("t", 1)
        add_eps("t", 1, ROWS)
        standardise_t(1, 0)
        standardise_t(1, 1)
        invert("t", 1)
        take_moments("t", 2, ROWS)
        standardise_t(2, 0)
        square_mean("t", 2)
        standardise_t(2, 1)
        bound_squares("t", 2)
        standardise_t(3, 0)
        subtract_mean("t", 2)
        standardise_t(3, 1)
        tanh_of_z(6, 0)
        tanh_of_z(6, 1)
        squares_of_tanh(6, 0)
        squares_of_tanh(6, 1)
        tanh_of_z(7, 0)
        tanh_of_z(7, 1)
        squares_of_tanh(7, 0)
        squares_of_tanh(7, 1)
        transpose_t(1, 0)
        transpose_t(1, 1)
        project_rel(0, 0)
        project_rel(0, 1)
        project_rel(1, 0)
        project_rel(1, 1)
        average("t", 3)
        take_root("t", 2)
        row_max(0, 0)
        row_max(0, 1)
        row_max(1, 0)
        add_eps("t", 2, ROWS)
        row_max(1, 1)
        invert("t", 2)
        take_moments("t", 3, ROWS)
        standardise_t(4, 0)
        square_mean("t", 3)
        standardise_t(4, 1)
        bound_squares("t", 3)
        standardise_t(5, 0)
        subtract_mean("t", 3)
        standardise_t(5, 1)
        row_exp_sum(0, 0)
        row_exp_sum(0, 1)
        row_exp_sum(1, 0)
        row_exp_sum(1, 1)
        regroup_t(0)
        regroup_t(1)
        project_rel(2, 0)
        project_rel(2, 1)
        transpose_t(2, 0)
        transpose_t(2, 1)
        project_rel(3, 0)
        project_rel(3, 1)
        transpose_t(3, 0)
        transpose_t(3, 1)
        transpose_t(4, 0)
        transpose_t(4, 1)
        take_root("t", 3)
        row_max(2, 0)
        row_max(2, 1)
        row_max(3, 0)
        add_eps("t", 3, ROWS)
        row_max(3, 1)
        invert("t", 3)
        standardise_t(6, 0)
        standardise_t(6, 1)
        standardise_t(7, 0)
        standardise_t(7, 1)
        row_exp_sum(2, 0)
        row_exp_sum(2, 1)
        regroup_t(2)
        regroup_t(3)
        row_exp_sum(3, 0)
        row_exp_sum(3, 1)
        regroup_t(4)
        project_rel(4, 0)
        project_rel(4, 1)
        transpose_t(5, 0)
        transpose_t(5, 1)
        project_rel(5, 0)
        project_rel(5, 1)
        transpose_t(6, 0)
        transpose_t(6, 1)
        transpose_t(7, 0)
        transpose_t(7, 1)
        quantise_t(0, 0)
        row_max(4, 0)
        quantise_t(0, 1)
        row_max(4, 1)
        row_max(5, 0)
        row_max(5, 1)
        regroup_t(5)
        row_exp_sum(4, 0)
        regroup_t(6)
        regroup_t(7)
        row_exp_sum(4, 1)
        second_product(0, 0)
        second_product(0, 1)
        project_rel(6, 0)
        project_rel(6, 1)
        quantise_t(1, 0)
        quantise_t(1, 1)
        tanh_of_u(0)
        squares_of_u(0)
        row_exp_sum(5, 0)
        row_exp_sum(5, 1)
        second_product(1, 0)
        second_product(1, 1)
        project_rel(7, 0)
        project_rel(7, 1)
        sum_u(0)
        row_max(6, 0)
        sum_squares_of_u(0)
        row_max(6, 1)
        row_max(7, 0)
        row_max(7, 1)
        tanh_of_u(1)
        squares_of_u(1)
        row_exp_sum(6, 0)
        row_exp_sum(6, 1)
        row_exp_sum(7, 0)
        row_exp_sum(7, 1)
        average("u", 0)
        turn_maxima()
        sum_u(1)
        sum_squares_of_u(1)
        take_moments("u", 0, WIDTH)
        join_maxima()
        shift_by_maxima()
        square_mean("u", 0)
        bound_squares("u", 0)
        rescale_by_maxima()
        load_sqrt()
        average("u", 1)
        turn_sums()
        take_moments("u", 1, WIDTH)
        subtract_mean("u", 0)
        square_mean("u", 1)
        rescale_sums()
        bound_squares("u", 1)
        total_mass()
        subtract_mean("u", 1)
        centre_u(0)
        invert_total()
        centre_u(1)
        take_root("u", 0)
        take_root("u", 1)
        add_eps("u", 0, WIDTH)
        add_eps("u", 1, WIDTH)
        invert("u", 0)
        invert("u", 1)
        store_mass()
        store_proj(0)
        store_proj(1)
